import numpy as np
import ml_dtypes


def mxq(x, axis, fmt="e4m3"):
    dtype, down = {"e4m3": (ml_dtypes.float8_e4m3fn, 7), "e5m2": (ml_dtypes.float8_e5m2, 14)}[fmt]
    v = np.moveaxis(np.asarray(x, np.float32).astype(ml_dtypes.bfloat16).astype(np.float64), axis, -1)
    blocks = v.reshape(v.shape[:-1] + (-1, 32))
    amax = np.abs(blocks).max(-1, keepdims=True)
    byte = np.maximum(np.where(amax > 0, np.frexp(amax)[1] - 1 + 127, 0) - down, 1)
    scale = np.exp2(byte - 127.0)
    codes = (blocks / scale).astype(np.float32).astype(dtype).astype(np.float64)
    return np.moveaxis((codes * scale).reshape(v.shape), -1, axis)


WIDE = False


def mx_kscale(k):
    if not WIDE:
        return np.ones(k)
    levels = np.array([10, -10, 5, -5, 0])
    a = np.random.permutation(np.resize(levels, k // 512 * 4)).reshape(k // 512, 4)
    idx = np.arange(k)
    return np.exp2(a[idx // 512, idx % 128 // 32])


BF16 = ml_dtypes.bfloat16


def bf(x):
    return np.asarray(x, np.float32).astype(BF16)


def f64(x):
    return np.asarray(x).astype(np.float64)


B, IN_DIM, HID, ATT = 16384, 128, 128, 256
TOTAL = IN_DIM + HID + ATT


def softplus(v):
    return np.logaddexp(v, 0.0)


def sigmoid(v):
    return 1.0 / (1.0 + np.exp(-v))


def setup_inputs():
    s = np.array(mx_kscale(TOTAL), np.float64)
    s[IN_DIM:IN_DIM + HID] = 1.0
    return {"t": 0.0,
            "h_ltc": bf(np.random.standard_normal((B, HID))),
            "x_t": bf(np.random.standard_normal((B, IN_DIM)) * s[:IN_DIM]),
            "context": bf(np.random.standard_normal((B, ATT)) * s[IN_DIM + HID:]),
            "W_gd": bf(np.random.uniform(-1.0, 1.0, (2 * HID, TOTAL)) * 3.0 / np.sqrt(TOTAL) / s[None, :]),
            "b_gd": bf(np.random.uniform(-0.1, 0.1, (2 * HID,))),
            "W_tau": bf(np.random.uniform(-1.0, 1.0, (HID, HID)) * 2.0 / np.sqrt(HID)),
            "b_tau": bf(np.random.uniform(-0.1, 0.1, (HID,))),
            "gleak": bf(np.random.uniform(0.001, 1.0, (HID,))),
            "cm": bf(np.random.uniform(0.4, 0.6, (HID,)))}


def reference(t, h_ltc, x_t, context, W_gd, b_gd, W_tau, b_tau, gleak, cm):
    h = f64(h_ltc)
    combined = np.concatenate([f64(x_t), h, f64(context)], axis=1)
    g_d = (mxq(combined, 1, "e4m3") @ mxq(f64(W_gd), 1, "e4m3").T) + f64(b_gd)
    gate, dynamics = np.split(g_d, 2, axis=1)
    tau = softplus(h @ f64(W_tau).T + f64(b_tau))
    numerator = sigmoid(gate) * np.tanh(dynamics) - h
    denominator = tau + softplus(f64(cm)) + softplus(f64(gleak))
    return numerator / (denominator + 1e-6)

@@ -1,0 +1,289 @@
+import math
+from contextlib import ExitStack
+
+import concourse.mybir as mybir
+from concourse.masks import make_identity
+
+F32 = mybir.dt.float32
+BF16 = mybir.dt.bfloat16
+U32 = mybir.dt.uint32
+U8 = mybir.dt.uint8
+FP8X4 = mybir.dt.float8_e4m3fn_x4
+ACT = mybir.ActivationFunctionType
+ALU = mybir.AluOpType
+
+P = 128
+B, IN_DIM, HID, ATT = 16384, 128, 128, 256
+K = IN_DIM + HID + ATT
+SLOTS = B // P
+CH = 512
+NCH = B // CH
+GS = 8
+NG = SLOTS // GS
+HS = 16
+NB = SLOTS // HS
+LAG = 2
+
+FLOPS = 2 * B * K * 2 * HID + 2 * B * HID * HID
+
+
+def tile_ltcattentioncell_t_kernel(
+    tc, t, h_ltc, x_t, context, W_gd, b_gd, W_tau, b_tau, gleak, cm, out
+):
+    nc = tc.nc
+    hv = h_ltc.rearrange("(p s) k -> p s k", s=SLOTS)
+    xv = x_t.rearrange("(p s) k -> p s k", s=SLOTS)
+    cv = context.rearrange("(p s) k -> p s k", s=SLOTS)
+    ov = out.rearrange("(p s) f -> p s f", s=SLOTS)
+
+    with ExitStack() as ctx:
+        const = ctx.enter_context(tc.tile_pool(name="const", bufs=1))
+        keep = ctx.enter_context(tc.tile_pool(name="keep", bufs=1))
+        hpool = ctx.enter_context(tc.tile_pool(name="hpool", bufs=4))
+        big = ctx.enter_context(tc.tile_pool(name="big", bufs=4))
+        mid = ctx.enter_context(tc.tile_pool(name="mid", bufs=3))
+        small = ctx.enter_context(tc.tile_pool(name="small", bufs=3))
+        psx = ctx.enter_context(tc.psum_pool(name="psx", bufs=4))
+        psa = ctx.enter_context(tc.psum_pool(name="psa", bufs=2))
+        psb = ctx.enter_context(tc.psum_pool(name="psb", bufs=2))
+        ctx.enter_context(tc.manual_schedule())
+
+        identb = const.tile([P, P], BF16, name="identb")
+        identf = const.tile([P, P], F32, name="identf")
+        make_identity(nc, identb[:])
+        make_identity(nc, identf[:])
+        brow = const.tile([P, P], BF16, name="brow")
+        nc.vector.memset(brow[:], 0.0)
+
+        htiles = {}
+
+        def load_h(b):
+            ht = hpool.tile([P, HS, HID], BF16, name="ht", tag="h")
+            nc.sync.dma_start(out=ht[:], in_=hv[:, b * HS : (b + 1) * HS, :])
+            htiles[b] = ht
+
+        load_h(0)
+        wtau = const.tile([P, HID], BF16, name="wtau")
+        nc.sync.dma_start(out=wtau[:], in_=W_tau)
+        nc.sync.dma_start(out=brow[0:2, :], in_=b_gd.rearrange("(a k) -> a k", a=2))
+        nc.sync.dma_start(out=brow[2:3, :], in_=b_tau.rearrange("(a k) -> a k", a=1))
+        nc.sync.dma_start(out=brow[3:4, :], in_=gleak.rearrange("(a k) -> a k", a=1))
+        nc.sync.dma_start(out=brow[4:5, :], in_=cm.rearrange("(a k) -> a k", a=1))
+        for b in range(1, 4):
+            load_h(b)
+
+        sp = psa.tile([P, 2 * P], BF16, name="sp", tag="a")
+        nc.tensor.transpose(out=sp[:, 0:P], in_=wtau[:], identity=identb[:])
+        nc.tensor.transpose(out=sp[:, P : 2 * P], in_=brow[:], identity=identb[:])
+        wtT = const.tile([P, HID], BF16, name="wtT")
+        nc.vector.tensor_copy(out=wtT[:], in_=sp[:, 0:P])
+        bcol = const.tile([P, 8], F32, name="bcol")
+        nc.vector.tensor_copy(out=bcol[:], in_=sp[:, P : P + 8])
+        nbt = const.tile([P, 1], F32, name="nbt")
+        nc.vector.tensor_scalar_mul(nbt[:], bcol[:, 2:3], -1.0)
+
+        tau = [keep.tile([P, 4 * CH], F32, name="tau%d" % b) for b in range(NB)]
+        codes = [
+            keep.tile([P, CH], U32, name="codes%d" % c, align_bytes=64) for c in range(NCH)
+        ]
+        planes = [
+            keep.tile([P, CH], U8, name="plane%d" % c, align_bytes=64) for c in range(NCH)
+        ]
+
+        hTs = {}
+
+        def h_transposes(u):
+            hp = psa.tile([P, 2 * CH], BF16, name="hp", tag="a")
+            src = htiles[u // 2]
+            for j in range(GS):
+                nc.tensor.transpose(
+                    out=hp[:, j * P : (j + 1) * P],
+                    in_=src[:, (u % 2) * GS + j, :],
+                    identity=identb[:],
+                )
+            hT = small.tile([P, 2 * CH], BF16, name="hT", tag="hT")
+            nc.vector.tensor_copy(out=hT[:], in_=hp[:])
+            hTs[u] = hT
+
+        def tau_chunk(c):
+            z = psx.tile([P, CH], F32, name="z", tag="x")
+            nc.tensor.matmul(
+                out=z[:],
+                lhsT=wtT[:],
+                rhs=hTs[c // 2][:, (c % 2) * CH : (c % 2 + 1) * CH],
+                start=True,
+                stop=True,
+            )
+            nc.scalar.activation(
+                out=tau[c // 4][:, (c % 4) * CH : (c % 4 + 1) * CH],
+                in_=z[:],
+                func=ACT.Sigmoid,
+                bias=nbt[:, 0:1],
+                scale=-1.0,
+            )
+
+        h_transposes(0)
+        h_transposes(1)
+        load_h(4)
+        for u in range(NG):
+            tau_chunk(2 * u)
+            tau_chunk(2 * u + 1)
+            if u + 2 < NG:
+                h_transposes(u + 2)
+                if u % 2 == 1 and (u + 1) // 2 + 4 < NB:
+                    load_h((u + 1) // 2 + 4)
+
+        sg = const.tile([P, 2], F32, name="sg")
+        nc.scalar.activation(out=sg[:], in_=bcol[:, 3:5], func=ACT.Sigmoid, scale=-1.0)
+        kap = const.tile([P, 1], F32, name="kap")
+        nc.vector.tensor_tensor(out=kap[:], in0=sg[:, 0:1], in1=sg[:, 1:2], op=ALU.mult)
+        nc.vector.tensor_scalar_mul(kap[:], kap[:], math.exp(-1e-6))
+
+        wraw = const.tile([P, 2, K], BF16, name="wraw")
+        nc.sync.dma_start(out=wraw[:], in_=W_gd.rearrange("(a p) k -> p a k", p=P))
+        combs = {}
+
+        def load_comb(g):
+            cb = big.tile([P, GS, K], BF16, name="comb", tag="big")
+            sl = slice(g * GS, (g + 1) * GS)
+            nc.sync.dma_start(out=cb[:, :, 0:IN_DIM], in_=xv[:, sl, :])
+            nc.sync.dma_start(out=cb[:, :, IN_DIM : IN_DIM + HID], in_=hv[:, sl, :])
+            nc.sync.dma_start(out=cb[:, :, IN_DIM + HID : K], in_=cv[:, sl, :])
+            combs[g] = cb
+
+        for g in range(4):
+            load_comb(g)
+
+        def ln_den(b):
+            nc.scalar.activation(out=tau[b][:], in_=tau[b][:], func=ACT.Ln, scale=kap[:, 0:1])
+
+        def ln_ln(b):
+            nc.scalar.activation(out=tau[b][:], in_=tau[b][:], func=ACT.Ln, scale=-1.0)
+
+        ln_den(0)
+        for b in range(NB):
+            if b + 1 < NB:
+                ln_den(b + 1)
+            ln_ln(b)
+        for b in range(NB):
+            nc.scalar.activation(out=tau[b][:], in_=tau[b][:], func=ACT.Exp, scale=-1.0)
+
+        def word_transposes(src, s0):
+            words = src[:].bitcast(F32).rearrange("p s (w u) -> p s u w", u=2)
+            xt = psx.tile([P, 2, 2 * P], F32, name="xt", tag="x")
+            for jj in range(2):
+                for u in range(2):
+                    nc.tensor.transpose(
+                        out=xt[:, u, jj * P : (jj + 1) * P],
+                        in_=words[:, s0 + jj, u, :],
+                        identity=identf[:],
+                    )
+            return xt
+
+        def regroup(xt, grouped, half):
+            dst = grouped[:].bitcast(F32).rearrange("p (c u) -> p c u", u=2)
+            nc.vector.tensor_copy(
+                out=dst[:, half * 2 * P : (half + 1) * 2 * P, :],
+                in_=xt[:].rearrange("p u c -> p c u"),
+            )
+
+        wgrp = const.tile([P, 4 * 2 * HID], BF16, name="wgrp", align_bytes=64)
+        wcodes = const.tile([P, 2 * HID], U32, name="wcodes", align_bytes=64)
+        wplane = const.tile([P, 2 * HID], U8, name="wplane", align_bytes=64)
+        regroup(word_transposes(wraw, 0), wgrp, 0)
+
+        groupeds = {}
+
+        def quantise(c):
+            nc.vector.quantize_mx(
+                out=codes[c][:].bitcast(FP8X4), scales=planes[c][:], in_=groupeds[c][:]
+            )
+
+        for c in range(NCH):
+            groupeds[c] = mid.tile([P, 4 * CH], BF16, name="grouped", tag="mid", align_bytes=64)
+            for half in range(2):
+                xt = word_transposes(combs[c // 2], (c % 2) * 4 + half * 2)
+                regroup(xt, groupeds[c], half)
+            if c == 0:
+                nc.vector.quantize_mx(
+                    out=wcodes[:].bitcast(FP8X4), scales=wplane[:], in_=wgrp[:]
+                )
+            else:
+                quantise(c - 1)
+            if c % 2 == 1 and c // 2 + 4 < NG:
+                load_comb(c // 2 + 4)
+        quantise(NCH - 1)
+        for b in range(4):
+            load_h(b)
+
+        sts = {}
+        outs = {}
+
+        def gates(c):
+            if c % 2 == 0:
+                sts[c // 2] = big.tile([P, 4, CH], F32, name="st", tag="big")
+            st = sts[c // 2]
+            for i in range(2):
+                g = psx.tile([P, CH], F32, name="g", tag="x")
+                nc.tensor.matmul_mx(
+                    out=g[:],
+                    lhsT=wcodes[:, i * HID : (i + 1) * HID].bitcast(FP8X4),
+                    lhsT_scale=wplane[:, i * HID : (i + 1) * HID],
+                    rhs=codes[c][:].bitcast(FP8X4),
+                    rhs_scale=planes[c][:],
+                    start=True,
+                    stop=True,
+                )
+                nc.scalar.activation(
+                    out=st[:, 2 * (c % 2) + i, :],
+                    in_=g[:],
+                    func=(ACT.Sigmoid if i == 0 else ACT.Tanh),
+                    bias=bcol[:, i : i + 1],
+                )
+
+        def product(c):
+            st = sts[c // 2]
+            a = st[:, 2 * (c % 2), :]
+            nc.gpsimd.tensor_tensor(out=a, in0=a, in1=st[:, 2 * (c % 2) + 1, :], op=ALU.mult)
+
+        def finish(c):
+            a = sts[c // 2][:, 2 * (c % 2), :]
+            r = tau[c // 4][:, (c % 4) * CH : (c % 4 + 1) * CH]
+            at = psa.tile([P, CH], F32, name="at", tag="a")
+            rt = psb.tile([P, CH], F32, name="rt", tag="b")
+            for j in range(4):
+                nc.tensor.transpose(
+                    out=at[:, j * P : (j + 1) * P], in_=a[:, j * P : (j + 1) * P], identity=identf[:]
+                )
+            for j in range(4):
+                nc.tensor.transpose(
+                    out=rt[:, j * P : (j + 1) * P], in_=r[:, j * P : (j + 1) * P], identity=identf[:]
+                )
+            if c % 2 == 0:
+                outs[c // 2] = mid.tile([P, 2 * CH], F32, name="o", tag="mid", align_bytes=64)
+            num = small.tile([P, CH], F32, name="num", tag="num")
+            hn = htiles[c // 4][:, (c % 4) * 4 : (c % 4 + 1) * 4, :].rearrange("p s k -> p (s k)")
+            nc.vector.tensor_tensor(out=num[:], in0=at[:], in1=hn, op=ALU.subtract)
+            nc.vector.tensor_tensor(
+                out=outs[c // 2][:, (c % 2) * CH : (c % 2 + 1) * CH],
+                in0=rt[:],
+                in1=num[:],
+                op=ALU.mult,
+            )
+            if c % 2 == 1:
+                nc.sync.dma_start(
+                    out=ov[:, (c // 2) * GS : (c // 2 + 1) * GS, :],
+                    in_=outs[c // 2][:].rearrange("p (s f) -> p s f", f=HID),
+                )
+            if c % 4 == 3 and c // 4 + 4 < NB:
+                load_h(c // 4 + 4)
+
+        for u in range(NG + LAG):
+            if u < NG:
+                gates(2 * u)
+                gates(2 * u + 1)
+                product(2 * u)
+                product(2 * u + 1)
+            if u >= LAG:
+                finish(2 * (u - LAG))
+                finish(2 * (u - LAG) + 1)

@@ -22,7 +22,16 @@ GS = 8
 NG = SLOTS // GS
 HS = 16
 NB = SLOTS // HS
-LAG = 2
+SH = 2
+PAIR_PROD = False
+S_EVERY = 13
+S_PHASE = 3
+REC_LATE = 4096
+REC_STEP = 256
+UP = 2.0 ** 20
+HB = 1024
+JOB_LEAD = 2
+NBIG = 3
 
 FLOPS = 2 * B * K * 2 * HID + 2 * B * HID * HID
 
@@ -39,10 +48,9 @@ def tile_ltcattentioncell_t_kernel(
     with ExitStack() as ctx:
         const = ctx.enter_context(tc.tile_pool(name="const", bufs=1))
         keep = ctx.enter_context(tc.tile_pool(name="keep", bufs=1))
-        hpool = ctx.enter_context(tc.tile_pool(name="hpool", bufs=4))
-        big = ctx.enter_context(tc.tile_pool(name="big", bufs=4))
+        big = ctx.enter_context(tc.tile_pool(name="big", bufs=NBIG))
         mid = ctx.enter_context(tc.tile_pool(name="mid", bufs=3))
-        small = ctx.enter_context(tc.tile_pool(name="small", bufs=3))
+        small = ctx.enter_context(tc.tile_pool(name="small", bufs=2))
         psx = ctx.enter_context(tc.psum_pool(name="psx", bufs=4))
         psa = ctx.enter_context(tc.psum_pool(name="psa", bufs=2))
         psb = ctx.enter_context(tc.psum_pool(name="psb", bufs=2))
@@ -55,22 +63,21 @@ def tile_ltcattentioncell_t_kernel(
         brow = const.tile([P, P], BF16, name="brow")
         nc.vector.memset(brow[:], 0.0)
 
-        htiles = {}
+        htiles = [keep.tile([P, HS, HID], BF16, name="ht%d" % b) for b in range(NB)]
 
-        def load_h(b):
-            ht = hpool.tile([P, HS, HID], BF16, name="ht", tag="h")
-            nc.sync.dma_start(out=ht[:], in_=hv[:, b * HS : (b + 1) * HS, :])
-            htiles[b] = ht
+        def load_h(b, s0, s1):
+            nc.sync.dma_start(out=htiles[b][:, s0:s1, :], in_=hv[:, b * HS + s0 : b * HS + s1, :])
 
-        load_h(0)
+        load_h(0, 0, GS)
         wtau = const.tile([P, HID], BF16, name="wtau")
         nc.sync.dma_start(out=wtau[:], in_=W_tau)
         nc.sync.dma_start(out=brow[0:2, :], in_=b_gd.rearrange("(a k) -> a k", a=2))
         nc.sync.dma_start(out=brow[2:3, :], in_=b_tau.rearrange("(a k) -> a k", a=1))
         nc.sync.dma_start(out=brow[3:4, :], in_=gleak.rearrange("(a k) -> a k", a=1))
         nc.sync.dma_start(out=brow[4:5, :], in_=cm.rearrange("(a k) -> a k", a=1))
-        for b in range(1, 4):
-            load_h(b)
+        load_h(0, GS, HS)
+        for b in range(1, NB):
+            load_h(b, 0, HS)
 
         sp = psa.tile([P, 2 * P], BF16, name="sp", tag="a")
         nc.tensor.transpose(out=sp[:, 0:P], in_=wtau[:], identity=identb[:])
@@ -79,6 +86,8 @@ def tile_ltcattentioncell_t_kernel(
         nc.vector.tensor_copy(out=wtT[:], in_=sp[:, 0:P])
         bcol = const.tile([P, 8], F32, name="bcol")
         nc.vector.tensor_copy(out=bcol[:], in_=sp[:, P : P + 8])
+        minus1 = const.tile([P, 1], F32, name="minus1")
+        nc.vector.memset(minus1[:], -1.0)
         nbt = const.tile([P, 1], F32, name="nbt")
         nc.vector.tensor_scalar_mul(nbt[:], bcol[:, 2:3], -1.0)
 
@@ -124,14 +133,11 @@ def tile_ltcattentioncell_t_kernel(
 
         h_transposes(0)
         h_transposes(1)
-        load_h(4)
         for u in range(NG):
             tau_chunk(2 * u)
             tau_chunk(2 * u + 1)
             if u + 2 < NG:
                 h_transposes(u + 2)
-                if u % 2 == 1 and (u + 1) // 2 + 4 < NB:
-                    load_h((u + 1) // 2 + 4)
 
         sg = const.tile([P, 2], F32, name="sg")
         nc.scalar.activation(out=sg[:], in_=bcol[:, 3:5], func=ACT.Sigmoid, scale=-1.0)
@@ -147,30 +153,53 @@ def tile_ltcattentioncell_t_kernel(
             cb = big.tile([P, GS, K], BF16, name="comb", tag="big")
             sl = slice(g * GS, (g + 1) * GS)
             nc.sync.dma_start(out=cb[:, :, 0:IN_DIM], in_=xv[:, sl, :])
-            nc.sync.dma_start(out=cb[:, :, IN_DIM : IN_DIM + HID], in_=hv[:, sl, :])
             nc.sync.dma_start(out=cb[:, :, IN_DIM + HID : K], in_=cv[:, sl, :])
+            nc.vector.tensor_copy(
+                out=cb[:, :, IN_DIM : IN_DIM + HID],
+                in_=htiles[g // 2][:, (g % 2) * GS : (g % 2 + 1) * GS, :],
+            )
             combs[g] = cb
 
-        for g in range(4):
+        for g in range(NBIG):
             load_comb(g)
 
-        def ln_den(b):
-            nc.scalar.activation(out=tau[b][:], in_=tau[b][:], func=ACT.Ln, scale=kap[:, 0:1])
+        def tau_part(j):
+            per = 4 * CH // HB
+            return tau[j // per][:, (j % per) * HB : (j % per + 1) * HB]
 
-        def ln_ln(b):
-            nc.scalar.activation(out=tau[b][:], in_=tau[b][:], func=ACT.Ln, scale=-1.0)
+        def job_ln(j):
+            nc.scalar.activation(out=tau_part(j), in_=tau_part(j), func=ACT.Ln, scale=kap[:, 0:1])
 
-        ln_den(0)
-        for b in range(NB):
-            if b + 1 < NB:
-                ln_den(b + 1)
-            ln_ln(b)
-        for b in range(NB):
-            nc.scalar.activation(out=tau[b][:], in_=tau[b][:], func=ACT.Exp, scale=-1.0)
+        def job_ln_up(j):
+            nc.scalar.activation(
+                out=tau_part(j), in_=tau_part(j), func=ACT.Ln, scale=-UP, bias=minus1[:, 0:1]
+            )
+
+        def rec_cols(c0, c1):
+            b = c0 // (4 * CH)
+            part = tau[b][:, c0 - b * 4 * CH : c1 - b * 4 * CH]
+            nc.scalar.activation(out=part, in_=part, func=ACT.Sigmoid, scale=-1.0)
+
+        def job_rec(j):
+            rec_cols(j * HB, (j + 1) * HB)
+
+        njob = B // HB
+        jobs = [(job_ln, 0)]
+        for j in range(njob):
+            if j + 1 < njob:
+                jobs.append((job_ln, j + 1))
+            jobs.append((job_ln_up, j))
+        for j in range((B - REC_LATE) // HB):
+            jobs.append((job_rec, j))
+
+        rings = [(psx, "x")] * 4 + [(psa, "a")] * 2 + [(psb, "b")] * 2
+        ring_pos = [0]
 
         def word_transposes(src, s0):
             words = src[:].bitcast(F32).rearrange("p s (w u) -> p s u w", u=2)
-            xt = psx.tile([P, 2, 2 * P], F32, name="xt", tag="x")
+            ring = rings[ring_pos[0] % len(rings)]
+            ring_pos[0] += 1
+            xt = ring[0].tile([P, 2, 2 * P], F32, name="xt", tag=ring[1])
             for jj in range(2):
                 for u in range(2):
                     nc.tensor.transpose(
@@ -180,17 +209,24 @@ def tile_ltcattentioncell_t_kernel(
                     )
             return xt
 
-        def regroup(xt, grouped, half):
+        def regroup(xt, grouped, half, on_scalar):
             dst = grouped[:].bitcast(F32).rearrange("p (c u) -> p c u", u=2)
-            nc.vector.tensor_copy(
-                out=dst[:, half * 2 * P : (half + 1) * 2 * P, :],
-                in_=xt[:].rearrange("p u c -> p c u"),
-            )
+            if on_scalar:
+                nc.scalar.copy(
+                    out=dst[:, half * 2 * P : (half + 1) * 2 * P, :],
+                    in_=xt[:].rearrange("p u c -> p c u"),
+                )
+            else:
+                nc.vector.tensor_copy(
+                    out=dst[:, half * 2 * P : (half + 1) * 2 * P, :],
+                    in_=xt[:].rearrange("p u c -> p c u"),
+                )
 
         wgrp = const.tile([P, 4 * 2 * HID], BF16, name="wgrp", align_bytes=64)
         wcodes = const.tile([P, 2 * HID], U32, name="wcodes", align_bytes=64)
         wplane = const.tile([P, 2 * HID], U8, name="wplane", align_bytes=64)
-        regroup(word_transposes(wraw, 0), wgrp, 0)
+        regroup(word_transposes(wraw, 0), wgrp, 0, False)
+        ring_pos[0] = 0
 
         groupeds = {}
 
@@ -199,22 +235,28 @@ def tile_ltcattentioncell_t_kernel(
                 out=codes[c][:].bitcast(FP8X4), scales=planes[c][:], in_=groupeds[c][:]
             )
 
+        done = 0
         for c in range(NCH):
             groupeds[c] = mid.tile([P, 4 * CH], BF16, name="grouped", tag="mid", align_bytes=64)
             for half in range(2):
+                k = 2 * c + half
+                while done < len(jobs) and done * 2 * NCH < (k + JOB_LEAD) * len(jobs):
+                    jobs[done][0](jobs[done][1])
+                    done += 1
                 xt = word_transposes(combs[c // 2], (c % 2) * 4 + half * 2)
-                regroup(xt, groupeds[c], half)
+                regroup(xt, groupeds[c], half, k % S_EVERY == S_PHASE)
             if c == 0:
                 nc.vector.quantize_mx(
                     out=wcodes[:].bitcast(FP8X4), scales=wplane[:], in_=wgrp[:]
                 )
             else:
                 quantise(c - 1)
-            if c % 2 == 1 and c // 2 + 4 < NG:
-                load_comb(c // 2 + 4)
+            if c % 2 == 1 and c // 2 + NBIG < NG:
+                load_comb(c // 2 + NBIG)
         quantise(NCH - 1)
-        for b in range(4):
-            load_h(b)
+        while done < len(jobs):
+            jobs[done][0](jobs[done][1])
+            done += 1
 
         sts = {}
         outs = {}
@@ -235,7 +277,7 @@ def tile_ltcattentioncell_t_kernel(
                     stop=True,
                 )
                 nc.scalar.activation(
-                    out=st[:, 2 * (c % 2) + i, :],
+                    out=st[:, 2 * i + c % 2, :],
                     in_=g[:],
                     func=(ACT.Sigmoid if i == 0 else ACT.Tanh),
                     bias=bcol[:, i : i + 1],
@@ -243,47 +285,60 @@ def tile_ltcattentioncell_t_kernel(
 
         def product(c):
             st = sts[c // 2]
-            a = st[:, 2 * (c % 2), :]
-            nc.gpsimd.tensor_tensor(out=a, in0=a, in1=st[:, 2 * (c % 2) + 1, :], op=ALU.mult)
+            if PAIR_PROD:
+                if c % 2 == 1:
+                    nc.gpsimd.tensor_tensor(
+                        out=st[:, 0:2, :], in0=st[:, 0:2, :], in1=st[:, 2:4, :], op=ALU.mult
+                    )
+            else:
+                a = st[:, c % 2, :]
+                nc.gpsimd.tensor_tensor(out=a, in0=a, in1=st[:, 2 + c % 2, :], op=ALU.mult)
 
         def finish(c):
-            a = sts[c // 2][:, 2 * (c % 2), :]
+            a = sts[c // 2][:, c % 2, :]
             r = tau[c // 4][:, (c % 4) * CH : (c % 4 + 1) * CH]
             at = psa.tile([P, CH], F32, name="at", tag="a")
             rt = psb.tile([P, CH], F32, name="rt", tag="b")
             for j in range(4):
                 nc.tensor.transpose(
-                    out=at[:, j * P : (j + 1) * P], in_=a[:, j * P : (j + 1) * P], identity=identf[:]
+                    out=rt[:, j * P : (j + 1) * P], in_=r[:, j * P : (j + 1) * P], identity=identf[:]
                 )
             for j in range(4):
                 nc.tensor.transpose(
-                    out=rt[:, j * P : (j + 1) * P], in_=r[:, j * P : (j + 1) * P], identity=identf[:]
+                    out=at[:, j * P : (j + 1) * P], in_=a[:, j * P : (j + 1) * P], identity=identf[:]
                 )
             if c % 2 == 0:
                 outs[c // 2] = mid.tile([P, 2 * CH], F32, name="o", tag="mid", align_bytes=64)
             num = small.tile([P, CH], F32, name="num", tag="num")
             hn = htiles[c // 4][:, (c % 4) * 4 : (c % 4 + 1) * 4, :].rearrange("p s k -> p (s k)")
             nc.vector.tensor_tensor(out=num[:], in0=at[:], in1=hn, op=ALU.subtract)
-            nc.vector.tensor_tensor(
+            nc.vector.scalar_tensor_tensor(
                 out=outs[c // 2][:, (c % 2) * CH : (c % 2 + 1) * CH],
                 in0=rt[:],
+                scalar=UP,
                 in1=num[:],
-                op=ALU.mult,
+                op0=ALU.mult,
+                op1=ALU.mult,
             )
             if c % 2 == 1:
                 nc.sync.dma_start(
                     out=ov[:, (c // 2) * GS : (c // 2 + 1) * GS, :],
                     in_=outs[c // 2][:].rearrange("p (s f) -> p s f", f=HID),
                 )
-            if c % 4 == 3 and c // 4 + 4 < NB:
-                load_h(c // 4 + 4)
 
-        for u in range(NG + LAG):
-            if u < NG:
-                gates(2 * u)
-                gates(2 * u + 1)
-                product(2 * u)
-                product(2 * u + 1)
-            if u >= LAG:
-                finish(2 * (u - LAG))
-                finish(2 * (u - LAG) + 1)
+        nfin = 0
+        late = B - REC_LATE
+        for u in range(NG):
+            gates(2 * u)
+            gates(2 * u + 1)
+            product(2 * u)
+            product(2 * u + 1)
+            if late < B:
+                rec_cols(late, late + REC_STEP)
+                late += REC_STEP
+            while nfin <= 2 * u + 1 - SH:
+                finish(nfin)
+                nfin += 1
+        while nfin < NCH:
+            finish(nfin)
+            nfin += 1

@@ -22,7 +22,6 @@ GS = 8
 NG = SLOTS // GS
 HS = 16
 NB = SLOTS // HS
-SH = 2
 PAIR_PROD = False
 S_EVERY = 13
 S_PHASE = 3
@@ -31,6 +30,8 @@ REC_STEP = 256
 UP = 2.0 ** 20
 HB = 1024
 JOB_LEAD = 2
+H_MOD = 2
+H_DMA = 1
 NBIG = 3
 
 FLOPS = 2 * B * K * 2 * HID + 2 * B * HID * HID
@@ -100,6 +101,7 @@ def tile_ltcattentioncell_t_kernel(
         ]
 
         hTs = {}
+        zrings = [(psx, "x")] * 4 + [(psb, "b")] * 2
 
         def h_transposes(u):
             hp = psa.tile([P, 2 * CH], BF16, name="hp", tag="a")
@@ -115,7 +117,8 @@ def tile_ltcattentioncell_t_kernel(
             hTs[u] = hT
 
         def tau_chunk(c):
-            z = psx.tile([P, CH], F32, name="z", tag="x")
+            zr = zrings[c % len(zrings)]
+            z = zr[0].tile([P, CH], F32, name="z", tag=zr[1])
             nc.tensor.matmul(
                 out=z[:],
                 lhsT=wtT[:],
@@ -154,10 +157,13 @@ def tile_ltcattentioncell_t_kernel(
             sl = slice(g * GS, (g + 1) * GS)
             nc.sync.dma_start(out=cb[:, :, 0:IN_DIM], in_=xv[:, sl, :])
             nc.sync.dma_start(out=cb[:, :, IN_DIM + HID : K], in_=cv[:, sl, :])
-            nc.vector.tensor_copy(
-                out=cb[:, :, IN_DIM : IN_DIM + HID],
-                in_=htiles[g // 2][:, (g % 2) * GS : (g % 2 + 1) * GS, :],
-            )
+            if g % H_MOD < H_DMA:
+                nc.sync.dma_start(out=cb[:, :, IN_DIM : IN_DIM + HID], in_=hv[:, sl, :])
+            else:
+                nc.vector.tensor_copy(
+                    out=cb[:, :, IN_DIM : IN_DIM + HID],
+                    in_=htiles[g // 2][:, (g % 2) * GS : (g % 2 + 1) * GS, :],
+                )
             combs[g] = cb
 
         for g in range(NBIG):
@@ -294,51 +300,82 @@ def tile_ltcattentioncell_t_kernel(
                 a = st[:, c % 2, :]
                 nc.gpsimd.tensor_tensor(out=a, in0=a, in1=st[:, 2 + c % 2, :], op=ALU.mult)
 
-        def finish(c):
-            a = sts[c // 2][:, c % 2, :]
+        rts = {}
+        ats = {}
+
+        def back_r(c):
             r = tau[c // 4][:, (c % 4) * CH : (c % 4 + 1) * CH]
-            at = psa.tile([P, CH], F32, name="at", tag="a")
-            rt = psb.tile([P, CH], F32, name="rt", tag="b")
+            rts[c] = psb.tile([P, CH], F32, name="rt", tag="b")
             for j in range(4):
                 nc.tensor.transpose(
-                    out=rt[:, j * P : (j + 1) * P], in_=r[:, j * P : (j + 1) * P], identity=identf[:]
+                    out=rts[c][:, j * P : (j + 1) * P],
+                    in_=r[:, j * P : (j + 1) * P],
+                    identity=identf[:],
                 )
+
+        def back_a(c):
+            a = sts[c // 2][:, c % 2, :]
+            ats[c] = psa.tile([P, CH], F32, name="at", tag="a")
             for j in range(4):
                 nc.tensor.transpose(
-                    out=at[:, j * P : (j + 1) * P], in_=a[:, j * P : (j + 1) * P], identity=identf[:]
+                    out=ats[c][:, j * P : (j + 1) * P],
+                    in_=a[:, j * P : (j + 1) * P],
+                    identity=identf[:],
                 )
+
+        def numerator(c):
+            nums[c] = small.tile([P, CH], F32, name="num", tag="num")
+            hn = htiles[c // 4][:, (c % 4) * 4 : (c % 4 + 1) * 4, :].rearrange("p s k -> p (s k)")
+            nc.vector.tensor_tensor(out=nums[c][:], in0=ats[c][:], in1=hn, op=ALU.subtract)
+
+        def result(c, alone):
             if c % 2 == 0:
                 outs[c // 2] = mid.tile([P, 2 * CH], F32, name="o", tag="mid", align_bytes=64)
-            num = small.tile([P, CH], F32, name="num", tag="num")
-            hn = htiles[c // 4][:, (c % 4) * 4 : (c % 4 + 1) * 4, :].rearrange("p s k -> p (s k)")
-            nc.vector.tensor_tensor(out=num[:], in0=at[:], in1=hn, op=ALU.subtract)
+            o = outs[c // 2]
             nc.vector.scalar_tensor_tensor(
-                out=outs[c // 2][:, (c % 2) * CH : (c % 2 + 1) * CH],
-                in0=rt[:],
+                out=o[:, (c % 2) * CH : (c % 2 + 1) * CH],
+                in0=rts[c][:],
                 scalar=UP,
-                in1=num[:],
+                in1=nums[c][:],
                 op0=ALU.mult,
                 op1=ALU.mult,
             )
-            if c % 2 == 1:
+            if alone:
+                nc.sync.dma_start(
+                    out=ov[:, c * 4 : (c + 1) * 4, :],
+                    in_=o[:, (c % 2) * CH : (c % 2 + 1) * CH].rearrange("p (s f) -> p s f", f=HID),
+                )
+            elif c % 2 == 1:
                 nc.sync.dma_start(
                     out=ov[:, (c // 2) * GS : (c // 2 + 1) * GS, :],
-                    in_=outs[c // 2][:].rearrange("p (s f) -> p s f", f=HID),
+                    in_=o[:].rearrange("p (s f) -> p s f", f=HID),
                 )
 
-        nfin = 0
+        def finish_pair(v):
+            for c in (2 * v, 2 * v + 1):
+                back_r(c)
+                back_a(c)
+                numerator(c)
+                result(c, False)
+
+        nums = {}
         late = B - REC_LATE
         for u in range(NG):
             gates(2 * u)
             gates(2 * u + 1)
             product(2 * u)
             product(2 * u + 1)
-            if late < B:
+            if late < B - 2 * CH:
                 rec_cols(late, late + REC_STEP)
                 late += REC_STEP
-            while nfin <= 2 * u + 1 - SH:
-                finish(nfin)
-                nfin += 1
-        while nfin < NCH:
-            finish(nfin)
-            nfin += 1
+            if u >= 1:
+                finish_pair(u - 1)
+        for c in (NCH - 2, NCH - 1):
+            back_a(c)
+            numerator(c)
+        for c in (NCH - 2, NCH - 1):
+            while late < (c + 1) * CH:
+                rec_cols(late, late + REC_STEP)
+                late += REC_STEP
+            back_r(c)
+            result(c, True)

@@ -23,10 +23,10 @@ NG = SLOTS // GS
 HS = 16
 NB = SLOTS // HS
 PAIR_PROD = False
-S_EVERY = 13
+S_EVERY = 8
 S_PHASE = 3
-REC_LATE = 4096
-REC_STEP = 256
+REC_LATE = 10240
+REC_STEP = 640
 UP = 2.0 ** 20
 HB = 1024
 JOB_LEAD = 2
@@ -182,9 +182,12 @@ def tile_ltcattentioncell_t_kernel(
             )
 
         def rec_cols(c0, c1):
-            b = c0 // (4 * CH)
-            part = tau[b][:, c0 - b * 4 * CH : c1 - b * 4 * CH]
-            nc.scalar.activation(out=part, in_=part, func=ACT.Sigmoid, scale=-1.0)
+            while c0 < c1:
+                b = c0 // (4 * CH)
+                e = min(c1, (b + 1) * 4 * CH)
+                part = tau[b][:, c0 - b * 4 * CH : e - b * 4 * CH]
+                nc.scalar.activation(out=part, in_=part, func=ACT.Sigmoid, scale=-1.0)
+                c0 = e
 
         def job_rec(j):
             rec_cols(j * HB, (j + 1) * HB)
@@ -366,16 +369,15 @@ def tile_ltcattentioncell_t_kernel(
             product(2 * u)
             product(2 * u + 1)
             if late < B - 2 * CH:
-                rec_cols(late, late + REC_STEP)
-                late += REC_STEP
+                rec_cols(late, min(late + REC_STEP, B - 2 * CH))
+                late = min(late + REC_STEP, B - 2 * CH)
             if u >= 1:
                 finish_pair(u - 1)
         for c in (NCH - 2, NCH - 1):
             back_a(c)
             numerator(c)
         for c in (NCH - 2, NCH - 1):
-            while late < (c + 1) * CH:
-                rec_cols(late, late + REC_STEP)
-                late += REC_STEP
+            rec_cols(late, (c + 1) * CH)
+            late = (c + 1) * CH
             back_r(c)
             result(c, True)

@@ -23,13 +23,9 @@ NG = SLOTS // GS
 HS = 16
 NB = SLOTS // HS
 PAIR_PROD = False
-S_EVERY = 8
-S_PHASE = 3
-REC_LATE = 10240
-REC_STEP = 640
-UP = 2.0 ** 20
 HB = 1024
-JOB_LEAD = 2
+LN_STEPS = 21
+S_EVERY = 3
 H_MOD = 2
 H_DMA = 1
 NBIG = 3
@@ -87,8 +83,6 @@ def tile_ltcattentioncell_t_kernel(
         nc.vector.tensor_copy(out=wtT[:], in_=sp[:, 0:P])
         bcol = const.tile([P, 8], F32, name="bcol")
         nc.vector.tensor_copy(out=bcol[:], in_=sp[:, P : P + 8])
-        minus1 = const.tile([P, 1], F32, name="minus1")
-        nc.vector.memset(minus1[:], -1.0)
         nbt = const.tile([P, 1], F32, name="nbt")
         nc.vector.tensor_scalar_mul(nbt[:], bcol[:, 2:3], -1.0)
 
@@ -176,30 +170,18 @@ def tile_ltcattentioncell_t_kernel(
         def job_ln(j):
             nc.scalar.activation(out=tau_part(j), in_=tau_part(j), func=ACT.Ln, scale=kap[:, 0:1])
 
-        def job_ln_up(j):
-            nc.scalar.activation(
-                out=tau_part(j), in_=tau_part(j), func=ACT.Ln, scale=-UP, bias=minus1[:, 0:1]
-            )
+        def job_sq(j):
+            nc.gpsimd.tensor_tensor(out=tau_part(j), in0=tau_part(j), in1=tau_part(j), op=ALU.mult)
 
-        def rec_cols(c0, c1):
-            while c0 < c1:
-                b = c0 // (4 * CH)
-                e = min(c1, (b + 1) * 4 * CH)
-                part = tau[b][:, c0 - b * 4 * CH : e - b * 4 * CH]
-                nc.scalar.activation(out=part, in_=part, func=ACT.Sigmoid, scale=-1.0)
-                c0 = e
-
-        def job_rec(j):
-            rec_cols(j * HB, (j + 1) * HB)
+        def job_rs(j):
+            nc.scalar.activation(out=tau_part(j), in_=tau_part(j), func=ACT.Abs_reciprocal_sqrt)
 
         njob = B // HB
-        jobs = [(job_ln, 0)]
+        jobs_at = {}
         for j in range(njob):
-            if j + 1 < njob:
-                jobs.append((job_ln, j + 1))
-            jobs.append((job_ln_up, j))
-        for j in range((B - REC_LATE) // HB):
-            jobs.append((job_rec, j))
+            jobs_at.setdefault((j * LN_STEPS) // njob, []).extend([(job_ln, j), (job_sq, j)])
+        for j in range(njob):
+            jobs_at.setdefault(LN_STEPS + (j * (2 * NCH - LN_STEPS)) // njob, []).append((job_rs, j))
 
         rings = [(psx, "x")] * 4 + [(psa, "a")] * 2 + [(psb, "b")] * 2
         ring_pos = [0]
@@ -244,16 +226,14 @@ def tile_ltcattentioncell_t_kernel(
                 out=codes[c][:].bitcast(FP8X4), scales=planes[c][:], in_=groupeds[c][:]
             )
 
-        done = 0
         for c in range(NCH):
             groupeds[c] = mid.tile([P, 4 * CH], BF16, name="grouped", tag="mid", align_bytes=64)
             for half in range(2):
                 k = 2 * c + half
-                while done < len(jobs) and done * 2 * NCH < (k + JOB_LEAD) * len(jobs):
-                    jobs[done][0](jobs[done][1])
-                    done += 1
+                for job in jobs_at.get(k, []):
+                    job[0](job[1])
                 xt = word_transposes(combs[c // 2], (c % 2) * 4 + half * 2)
-                regroup(xt, groupeds[c], half, k % S_EVERY == S_PHASE)
+                regroup(xt, groupeds[c], half, k >= LN_STEPS and (k - LN_STEPS) % S_EVERY == 1)
             if c == 0:
                 nc.vector.quantize_mx(
                     out=wcodes[:].bitcast(FP8X4), scales=wplane[:], in_=wgrp[:]
@@ -263,9 +243,6 @@ def tile_ltcattentioncell_t_kernel(
             if c % 2 == 1 and c // 2 + NBIG < NG:
                 load_comb(c // 2 + NBIG)
         quantise(NCH - 1)
-        while done < len(jobs):
-            jobs[done][0](jobs[done][1])
-            done += 1
 
         sts = {}
         outs = {}
@@ -335,13 +312,11 @@ def tile_ltcattentioncell_t_kernel(
             if c % 2 == 0:
                 outs[c // 2] = mid.tile([P, 2 * CH], F32, name="o", tag="mid", align_bytes=64)
             o = outs[c // 2]
-            nc.vector.scalar_tensor_tensor(
+            nc.vector.tensor_tensor(
                 out=o[:, (c % 2) * CH : (c % 2 + 1) * CH],
                 in0=rts[c][:],
-                scalar=UP,
                 in1=nums[c][:],
-                op0=ALU.mult,
-                op1=ALU.mult,
+                op=ALU.mult,
             )
             if alone:
                 nc.sync.dma_start(
@@ -362,22 +337,15 @@ def tile_ltcattentioncell_t_kernel(
                 result(c, False)
 
         nums = {}
-        late = B - REC_LATE
         for u in range(NG):
             gates(2 * u)
             gates(2 * u + 1)
             product(2 * u)
             product(2 * u + 1)
-            if late < B - 2 * CH:
-                rec_cols(late, min(late + REC_STEP, B - 2 * CH))
-                late = min(late + REC_STEP, B - 2 * CH)
             if u >= 1:
                 finish_pair(u - 1)
         for c in (NCH - 2, NCH - 1):
+            back_r(c)
             back_a(c)
             numerator(c)
-        for c in (NCH - 2, NCH - 1):
-            rec_cols(late, (c + 1) * CH)
-            late = (c + 1) * CH
-            back_r(c)
             result(c, True)

@@ -24,8 +24,9 @@ HS = 16
 NB = SLOTS // HS
 PAIR_PROD = False
 HB = 1024
-LN_STEPS = 21
-S_EVERY = 3
+S_EVERY = 4
+S_PHASE = 3
+SQUARER = "GVSVGSVS"
 H_MOD = 2
 H_DMA = 1
 NBIG = 3
@@ -170,18 +171,14 @@ def tile_ltcattentioncell_t_kernel(
         def job_ln(j):
             nc.scalar.activation(out=tau_part(j), in_=tau_part(j), func=ACT.Ln, scale=kap[:, 0:1])
 
-        def job_sq(j):
-            nc.gpsimd.tensor_tensor(out=tau_part(j), in0=tau_part(j), in1=tau_part(j), op=ALU.mult)
-
         def job_rs(j):
             nc.scalar.activation(out=tau_part(j), in_=tau_part(j), func=ACT.Abs_reciprocal_sqrt)
 
         njob = B // HB
         jobs_at = {}
         for j in range(njob):
-            jobs_at.setdefault((j * LN_STEPS) // njob, []).extend([(job_ln, j), (job_sq, j)])
-        for j in range(njob):
-            jobs_at.setdefault(LN_STEPS + (j * (2 * NCH - LN_STEPS)) // njob, []).append((job_rs, j))
+            jobs_at[(j * NCH) // njob] = (job_ln, j)
+            jobs_at[NCH + (j * NCH) // njob] = (job_rs, j)
 
         rings = [(psx, "x")] * 4 + [(psa, "a")] * 2 + [(psb, "b")] * 2
         ring_pos = [0]
@@ -230,10 +227,10 @@ def tile_ltcattentioncell_t_kernel(
             groupeds[c] = mid.tile([P, 4 * CH], BF16, name="grouped", tag="mid", align_bytes=64)
             for half in range(2):
                 k = 2 * c + half
-                for job in jobs_at.get(k, []):
-                    job[0](job[1])
+                if k in jobs_at:
+                    jobs_at[k][0](jobs_at[k][1])
                 xt = word_transposes(combs[c // 2], (c % 2) * 4 + half * 2)
-                regroup(xt, groupeds[c], half, k >= LN_STEPS and (k - LN_STEPS) % S_EVERY == 1)
+                regroup(xt, groupeds[c], half, k % S_EVERY == S_PHASE)
             if c == 0:
                 nc.vector.quantize_mx(
                     out=wcodes[:].bitcast(FP8X4), scales=wplane[:], in_=wgrp[:]
@@ -280,6 +277,14 @@ def tile_ltcattentioncell_t_kernel(
                 a = st[:, c % 2, :]
                 nc.gpsimd.tensor_tensor(out=a, in0=a, in1=st[:, 2 + c % 2, :], op=ALU.mult)
 
+        def square(c):
+            r = tau[c // 4][:, (c % 4) * CH : (c % 4 + 1) * CH]
+            who = SQUARER[c % len(SQUARER)]
+            if who == "G":
+                nc.gpsimd.tensor_tensor(out=r, in0=r, in1=r, op=ALU.mult)
+            elif who == "S":
+                nc.scalar.activation(out=r, in_=r, func=ACT.Square)
+
         rts = {}
         ats = {}
 
@@ -307,6 +312,10 @@ def tile_ltcattentioncell_t_kernel(
             nums[c] = small.tile([P, CH], F32, name="num", tag="num")
             hn = htiles[c // 4][:, (c % 4) * 4 : (c % 4 + 1) * 4, :].rearrange("p s k -> p (s k)")
             nc.vector.tensor_tensor(out=nums[c][:], in0=ats[c][:], in1=hn, op=ALU.subtract)
+            if SQUARER[c % len(SQUARER)] == "V":
+                once = small.tile([P, CH], F32, name="once", tag="once")
+                nc.vector.tensor_tensor(out=once[:], in0=rts[c][:], in1=nums[c][:], op=ALU.mult)
+                nums[c] = once
 
         def result(c, alone):
             if c % 2 == 0:
@@ -342,6 +351,8 @@ def tile_ltcattentioncell_t_kernel(
             gates(2 * u + 1)
             product(2 * u)
             product(2 * u + 1)
+            square(2 * u)
+            square(2 * u + 1)
             if u >= 1:
                 finish_pair(u - 1)
         for c in (NCH - 2, NCH - 1):

@@ -24,12 +24,16 @@ HS = 16
 NB = SLOTS // HS
 PAIR_PROD = False
 HB = 1024
-S_EVERY = 4
+S_EVERY = 5
 S_PHASE = 3
-SQUARER = "GVSVGSVS"
+JOB_END = 56
+EARLY = (58, 62)
+SQ = "SVSVSVGS"
+TAIL_S = 6
+LAG = 2
 H_MOD = 2
 H_DMA = 1
-NBIG = 3
+NBIG = 4
 
 FLOPS = 2 * B * K * 2 * HID + 2 * B * HID * HID
 
@@ -60,6 +64,10 @@ def tile_ltcattentioncell_t_kernel(
         make_identity(nc, identf[:])
         brow = const.tile([P, P], BF16, name="brow")
         nc.vector.memset(brow[:], 0.0)
+
+        warm = const.tile([P, 1], F32, name="warm")
+        nc.vector.memset(warm[:], 0.0)
+        nc.scalar.activation(out=warm[:], in_=warm[:], func=ACT.Sigmoid)
 
         htiles = [keep.tile([P, HS, HID], BF16, name="ht%d" % b) for b in range(NB)]
 
@@ -177,8 +185,8 @@ def tile_ltcattentioncell_t_kernel(
         njob = B // HB
         jobs_at = {}
         for j in range(njob):
-            jobs_at[(j * NCH) // njob] = (job_ln, j)
-            jobs_at[NCH + (j * NCH) // njob] = (job_rs, j)
+            jobs_at[(j * JOB_END) // (2 * njob)] = (job_ln, j)
+            jobs_at[((j + njob) * JOB_END) // (2 * njob)] = (job_rs, j)
 
         rings = [(psx, "x")] * 4 + [(psa, "a")] * 2 + [(psb, "b")] * 2
         ring_pos = [0]
@@ -186,6 +194,8 @@ def tile_ltcattentioncell_t_kernel(
         def word_transposes(src, s0):
             words = src[:].bitcast(F32).rearrange("p s (w u) -> p s u w", u=2)
             ring = rings[ring_pos[0] % len(rings)]
+            if ring_pos[0] >= EARLY[0] - 3:
+                ring = rings[4 + ring_pos[0] % 4]
             ring_pos[0] += 1
             xt = ring[0].tile([P, 2, 2 * P], F32, name="xt", tag=ring[1])
             for jj in range(2):
@@ -215,31 +225,6 @@ def tile_ltcattentioncell_t_kernel(
         wplane = const.tile([P, 2 * HID], U8, name="wplane", align_bytes=64)
         regroup(word_transposes(wraw, 0), wgrp, 0, False)
         ring_pos[0] = 0
-
-        groupeds = {}
-
-        def quantise(c):
-            nc.vector.quantize_mx(
-                out=codes[c][:].bitcast(FP8X4), scales=planes[c][:], in_=groupeds[c][:]
-            )
-
-        for c in range(NCH):
-            groupeds[c] = mid.tile([P, 4 * CH], BF16, name="grouped", tag="mid", align_bytes=64)
-            for half in range(2):
-                k = 2 * c + half
-                if k in jobs_at:
-                    jobs_at[k][0](jobs_at[k][1])
-                xt = word_transposes(combs[c // 2], (c % 2) * 4 + half * 2)
-                regroup(xt, groupeds[c], half, k % S_EVERY == S_PHASE)
-            if c == 0:
-                nc.vector.quantize_mx(
-                    out=wcodes[:].bitcast(FP8X4), scales=wplane[:], in_=wgrp[:]
-                )
-            else:
-                quantise(c - 1)
-            if c % 2 == 1 and c // 2 + NBIG < NG:
-                load_comb(c // 2 + NBIG)
-        quantise(NCH - 1)
 
         sts = {}
         outs = {}
@@ -277,13 +262,15 @@ def tile_ltcattentioncell_t_kernel(
                 a = st[:, c % 2, :]
                 nc.gpsimd.tensor_tensor(out=a, in0=a, in1=st[:, 2 + c % 2, :], op=ALU.mult)
 
+        def who(c):
+            return "S" if c >= NCH - TAIL_S else SQ[c % 8]
+
         def square(c):
             r = tau[c // 4][:, (c % 4) * CH : (c % 4 + 1) * CH]
-            who = SQUARER[c % len(SQUARER)]
-            if who == "G":
-                nc.gpsimd.tensor_tensor(out=r, in0=r, in1=r, op=ALU.mult)
-            elif who == "S":
+            if who(c) == "S":
                 nc.scalar.activation(out=r, in_=r, func=ACT.Square)
+            elif who(c) == "G":
+                nc.gpsimd.tensor_tensor(out=r, in0=r, in1=r, op=ALU.mult)
 
         rts = {}
         ats = {}
@@ -312,13 +299,14 @@ def tile_ltcattentioncell_t_kernel(
             nums[c] = small.tile([P, CH], F32, name="num", tag="num")
             hn = htiles[c // 4][:, (c % 4) * 4 : (c % 4 + 1) * 4, :].rearrange("p s k -> p (s k)")
             nc.vector.tensor_tensor(out=nums[c][:], in0=ats[c][:], in1=hn, op=ALU.subtract)
-            if SQUARER[c % len(SQUARER)] == "V":
-                once = small.tile([P, CH], F32, name="once", tag="once")
-                nc.vector.tensor_tensor(out=once[:], in0=rts[c][:], in1=nums[c][:], op=ALU.mult)
-                nums[c] = once
+
+        def once(c):
+            first = small.tile([P, CH], F32, name="first", tag="hT")
+            nc.vector.tensor_tensor(out=first[:], in0=rts[c][:], in1=nums[c][:], op=ALU.mult)
+            nums[c] = first
 
         def result(c, alone):
-            if c % 2 == 0:
+            if c // 2 not in outs:
                 outs[c // 2] = mid.tile([P, 2 * CH], F32, name="o", tag="mid", align_bytes=64)
             o = outs[c // 2]
             nc.vector.tensor_tensor(
@@ -332,31 +320,68 @@ def tile_ltcattentioncell_t_kernel(
                     out=ov[:, c * 4 : (c + 1) * 4, :],
                     in_=o[:, (c % 2) * CH : (c % 2 + 1) * CH].rearrange("p (s f) -> p s f", f=HID),
                 )
-            elif c % 2 == 1:
-                nc.sync.dma_start(
-                    out=ov[:, (c // 2) * GS : (c // 2 + 1) * GS, :],
-                    in_=o[:].rearrange("p (s f) -> p s f", f=HID),
-                )
 
         def finish_pair(v):
-            for c in (2 * v, 2 * v + 1):
-                back_r(c)
-                back_a(c)
-                numerator(c)
-                result(c, False)
+            c0, c1 = 2 * v, 2 * v + 1
+            back_a(c1)
+            back_a(c0)
+            back_r(c1)
+            back_r(c0)
+            numerator(c1)
+            numerator(c0)
+            twice = [c for c in (c1, c0) if who(c) == "V"]
+            for c in twice:
+                once(c)
+            for c in (c1, c0):
+                if c not in twice:
+                    result(c, v == NG - 1)
+            for c in twice:
+                result(c, v == NG - 1)
+            if v < NG - 1:
+                nc.sync.dma_start(
+                    out=ov[:, v * GS : (v + 1) * GS, :],
+                    in_=outs[v][:].rearrange("p (s f) -> p s f", f=HID),
+                )
 
         nums = {}
-        for u in range(NG):
+
+        def start_pair(u):
             gates(2 * u)
             gates(2 * u + 1)
             product(2 * u)
             product(2 * u + 1)
             square(2 * u)
             square(2 * u + 1)
-            if u >= 1:
-                finish_pair(u - 1)
-        for c in (NCH - 2, NCH - 1):
-            back_r(c)
-            back_a(c)
-            numerator(c)
-            result(c, True)
+
+        groupeds = {}
+
+        def quantise(c):
+            nc.vector.quantize_mx(
+                out=codes[c][:].bitcast(FP8X4), scales=planes[c][:], in_=groupeds[c][:]
+            )
+
+        for c in range(NCH):
+            groupeds[c] = mid.tile([P, 4 * CH], BF16, name="grouped", tag="mid", align_bytes=64)
+            for half in range(2):
+                k = 2 * c + half
+                if k in jobs_at:
+                    jobs_at[k][0](jobs_at[k][1])
+                xt = word_transposes(combs[c // 2], (c % 2) * 4 + half * 2)
+                regroup(xt, groupeds[c], half, k % S_EVERY == S_PHASE and k < JOB_END)
+                if k in EARLY:
+                    start_pair(EARLY.index(k))
+            if c == 0:
+                nc.vector.quantize_mx(
+                    out=wcodes[:].bitcast(FP8X4), scales=wplane[:], in_=wgrp[:]
+                )
+            else:
+                quantise(c - 1)
+            if c % 2 == 1 and c // 2 + NBIG < NG:
+                load_comb(c // 2 + NBIG)
+        quantise(NCH - 1)
+
+        for u in range(len(EARLY), NG + LAG):
+            if u < NG:
+                start_pair(u)
+            if u >= LAG:
+                finish_pair(u - LAG)

@@ -28,7 +28,7 @@ S_EVERY = 5
 S_PHASE = 3
 JOB_END = 56
 EARLY = (58, 62)
-SQ = "SVSVSVGS"
+SQ = "SVSVSVSV"
 TAIL_S = 6
 LAG = 2
 H_MOD = 2

@@ -95,6 +95,9 @@ def tile_ltcattentioncell_t_kernel(
         nbt = const.tile([P, 1], F32, name="nbt")
         nc.vector.tensor_scalar_mul(nbt[:], bcol[:, 2:3], -1.0)
 
+        sg = const.tile([P, 2], F32, name="sg")
+        nc.scalar.activation(out=sg[:], in_=bcol[:, 3:5], func=ACT.Sigmoid, scale=-1.0)
+
         tau = [keep.tile([P, 4 * CH], F32, name="tau%d" % b) for b in range(NB)]
         codes = [
             keep.tile([P, CH], U32, name="codes%d" % c, align_bytes=64) for c in range(NCH)
@@ -139,17 +142,14 @@ def tile_ltcattentioncell_t_kernel(
 
         h_transposes(0)
         h_transposes(1)
+        kap = const.tile([P, 1], F32, name="kap")
+        nc.vector.tensor_tensor(out=kap[:], in0=sg[:, 0:1], in1=sg[:, 1:2], op=ALU.mult)
+        nc.vector.tensor_scalar_mul(kap[:], kap[:], math.exp(-1e-6))
         for u in range(NG):
             tau_chunk(2 * u)
             tau_chunk(2 * u + 1)
             if u + 2 < NG:
                 h_transposes(u + 2)
-
-        sg = const.tile([P, 2], F32, name="sg")
-        nc.scalar.activation(out=sg[:], in_=bcol[:, 3:5], func=ACT.Sigmoid, scale=-1.0)
-        kap = const.tile([P, 1], F32, name="kap")
-        nc.vector.tensor_tensor(out=kap[:], in0=sg[:, 0:1], in1=sg[:, 1:2], op=ALU.mult)
-        nc.vector.tensor_scalar_mul(kap[:], kap[:], math.exp(-1e-6))
 
         wraw = const.tile([P, 2, K], BF16, name="wraw")
         nc.sync.dma_start(out=wraw[:], in_=W_gd.rearrange("(a p) k -> p a k", p=P))

@@ -25,12 +25,20 @@ NB = SLOTS // HS
 PAIR_PROD = False
 HB = 1024
 S_EVERY = 5
-S_PHASE = 3
+S_PHASE = 2
 JOB_END = 56
-EARLY = (58, 62)
-SQ = "SVSVSVSV"
-TAIL_S = 6
-LAG = 2
+S_FROM = 8
+V_PROD = ()
+LAG2 = 2
+LAG_END = 11
+P_AT = 14
+EARLY = (56, 59, 62)
+SQ = "SDSDSDSD"
+TAIL_S = 4
+G_L = 9
+G_FIRST = 1
+GW = 512
+LAG = 3
 H_MOD = 2
 H_DMA = 1
 NBIG = 4
@@ -186,7 +194,7 @@ def tile_ltcattentioncell_t_kernel(
         jobs_at = {}
         for j in range(njob):
             jobs_at[(j * JOB_END) // (2 * njob)] = (job_ln, j)
-            jobs_at[((j + njob) * JOB_END) // (2 * njob)] = (job_rs, j)
+            jobs_at[((j + njob) * JOB_END) // (2 * njob)] = (job_rs, (j + G_L) % njob)
 
         rings = [(psx, "x")] * 4 + [(psa, "a")] * 2 + [(psb, "b")] * 2
         ring_pos = [0]
@@ -260,17 +268,17 @@ def tile_ltcattentioncell_t_kernel(
                     )
             else:
                 a = st[:, c % 2, :]
-                nc.gpsimd.tensor_tensor(out=a, in0=a, in1=st[:, 2 + c % 2, :], op=ALU.mult)
+                eng = nc.vector if c in V_PROD else nc.gpsimd
+                eng.tensor_tensor(out=a, in0=a, in1=st[:, 2 + c % 2, :], op=ALU.mult)
 
         def who(c):
-            return "S" if c >= NCH - TAIL_S else SQ[c % 8]
+            kind = "S" if c >= NCH - TAIL_S else SQ[c % 8]
+            return "S" if kind == "D" and c // 2 + G_FIRST >= P_AT else kind
 
         def square(c):
             r = tau[c // 4][:, (c % 4) * CH : (c % 4 + 1) * CH]
             if who(c) == "S":
                 nc.scalar.activation(out=r, in_=r, func=ACT.Square)
-            elif who(c) == "G":
-                nc.gpsimd.tensor_tensor(out=r, in0=r, in1=r, op=ALU.mult)
 
         rts = {}
         ats = {}
@@ -327,6 +335,9 @@ def tile_ltcattentioncell_t_kernel(
             back_a(c0)
             back_r(c1)
             back_r(c0)
+            for c in (2 * v + 2, 2 * v + 3):
+                if c in V_PROD:
+                    product(c)
             numerator(c1)
             numerator(c0)
             twice = [c for c in (c1, c0) if who(c) == "V"]
@@ -345,11 +356,12 @@ def tile_ltcattentioncell_t_kernel(
 
         nums = {}
 
-        def start_pair(u):
+        def start_pair(u, products=True):
             gates(2 * u)
             gates(2 * u + 1)
-            product(2 * u)
-            product(2 * u + 1)
+            for c in (2 * u, 2 * u + 1):
+                if products and c not in V_PROD:
+                    product(c)
             square(2 * u)
             square(2 * u + 1)
 
@@ -367,21 +379,33 @@ def tile_ltcattentioncell_t_kernel(
                 if k in jobs_at:
                     jobs_at[k][0](jobs_at[k][1])
                 xt = word_transposes(combs[c // 2], (c % 2) * 4 + half * 2)
-                regroup(xt, groupeds[c], half, k % S_EVERY == S_PHASE and k < JOB_END)
+                regroup(xt, groupeds[c], half, k % S_EVERY == S_PHASE and S_FROM <= k < JOB_END)
                 if k in EARLY:
-                    start_pair(EARLY.index(k))
+                    start_pair(EARLY.index(k), False)
             if c == 0:
                 nc.vector.quantize_mx(
                     out=wcodes[:].bitcast(FP8X4), scales=wplane[:], in_=wgrp[:]
                 )
-            else:
+            if c % 2 == 1:
                 quantise(c - 1)
+                quantise(c)
+                sq = c - 2 * G_FIRST
+                if c // 2 >= G_FIRST:
+                    tick = small.tile([P, 1], U32, name="tick", tag="tick")
+                    nc.gpsimd.tensor_copy(out=tick[:], in_=codes[c][:, 0:1])
+                if sq >= 0 and who(sq) == "D":
+                    r = tau[sq // 4][:, (sq % 4) * CH : (sq % 4 + 1) * CH]
+                    nc.gpsimd.tensor_tensor(out=r, in0=r, in1=r, op=ALU.mult)
+                if c // 2 == P_AT:
+                    product(0)
+                    product(1)
             if c % 2 == 1 and c // 2 + NBIG < NG:
                 load_comb(c // 2 + NBIG)
-        quantise(NCH - 1)
-
-        for u in range(len(EARLY), NG + LAG):
-            if u < NG:
-                start_pair(u)
-            if u >= LAG:
-                finish_pair(u - LAG)
+        for c in range(2 if P_AT < NG else 0, 2 * len(EARLY)):
+            product(c)
+        started = len(EARLY)
+        for v in range(NG):
+            while started < min(NG, v + 1 + (LAG if v < LAG_END else LAG2)):
+                start_pair(started)
+                started += 1
+            finish_pair(v)

@@ -27,7 +27,7 @@ HB = 1024
 S_EVERY = 5
 S_PHASE = 2
 JOB_END = 56
-S_FROM = 8
+S_FROM = 20
 V_PROD = ()
 LAG2 = 2
 LAG_END = 11
@@ -41,6 +41,10 @@ GW = 512
 LAG = 3
 H_MOD = 2
 H_DMA = 1
+WARM = 4
+W_AT = 13
+F_AT = {14: (0, 1), 15: ()}
+F_EARLY = 3
 NBIG = 4
 
 FLOPS = 2 * B * K * 2 * HID + 2 * B * HID * HID
@@ -61,50 +65,47 @@ def tile_ltcattentioncell_t_kernel(
         big = ctx.enter_context(tc.tile_pool(name="big", bufs=NBIG))
         mid = ctx.enter_context(tc.tile_pool(name="mid", bufs=3))
         small = ctx.enter_context(tc.tile_pool(name="small", bufs=2))
+        htp = ctx.enter_context(tc.tile_pool(name="htp", bufs=3))
         psx = ctx.enter_context(tc.psum_pool(name="psx", bufs=4))
         psa = ctx.enter_context(tc.psum_pool(name="psa", bufs=2))
         psb = ctx.enter_context(tc.psum_pool(name="psb", bufs=2))
         ctx.enter_context(tc.manual_schedule())
 
+        wbf = const.tile([P, CH], BF16, name="wbf")
+        nc.vector.memset(wbf[:], 0.0)
         identb = const.tile([P, P], BF16, name="identb")
         identf = const.tile([P, P], F32, name="identf")
         make_identity(nc, identb[:])
         make_identity(nc, identf[:])
         brow = const.tile([P, P], BF16, name="brow")
         nc.vector.memset(brow[:], 0.0)
+        brow2 = const.tile([P, P], BF16, name="brow2")
+        nc.vector.memset(brow2[:], 0.0)
 
+        for i in range(WARM):
+            wps = psx.tile([P, CH], F32, name="wps", tag="x")
+            nc.tensor.matmul(out=wps[:], lhsT=wbf[:, 0:P], rhs=wbf[:], start=True, stop=True)
         warm = const.tile([P, 1], F32, name="warm")
         nc.vector.memset(warm[:], 0.0)
-        nc.scalar.activation(out=warm[:], in_=warm[:], func=ACT.Sigmoid)
 
         htiles = [keep.tile([P, HS, HID], BF16, name="ht%d" % b) for b in range(NB)]
 
         def load_h(b, s0, s1):
             nc.sync.dma_start(out=htiles[b][:, s0:s1, :], in_=hv[:, b * HS + s0 : b * HS + s1, :])
 
-        load_h(0, 0, GS)
+        load_h(0, 0, GS // 2)
         wtau = const.tile([P, HID], BF16, name="wtau")
-        nc.sync.dma_start(out=wtau[:], in_=W_tau)
-        nc.sync.dma_start(out=brow[0:2, :], in_=b_gd.rearrange("(a k) -> a k", a=2))
-        nc.sync.dma_start(out=brow[2:3, :], in_=b_tau.rearrange("(a k) -> a k", a=1))
-        nc.sync.dma_start(out=brow[3:4, :], in_=gleak.rearrange("(a k) -> a k", a=1))
-        nc.sync.dma_start(out=brow[4:5, :], in_=cm.rearrange("(a k) -> a k", a=1))
+        nc.scalar.dma_start(out=wtau[:], in_=W_tau)
+        nc.scalar.dma_start(out=brow[0:1, :], in_=b_tau.rearrange("(a k) -> a k", a=1))
+        nc.scalar.activation(out=warm[:], in_=warm[:], func=ACT.Sigmoid)
+        load_h(0, GS // 2, GS)
         load_h(0, GS, HS)
         for b in range(1, NB):
             load_h(b, 0, HS)
-
-        sp = psa.tile([P, 2 * P], BF16, name="sp", tag="a")
-        nc.tensor.transpose(out=sp[:, 0:P], in_=wtau[:], identity=identb[:])
-        nc.tensor.transpose(out=sp[:, P : 2 * P], in_=brow[:], identity=identb[:])
-        wtT = const.tile([P, HID], BF16, name="wtT")
-        nc.vector.tensor_copy(out=wtT[:], in_=sp[:, 0:P])
-        bcol = const.tile([P, 8], F32, name="bcol")
-        nc.vector.tensor_copy(out=bcol[:], in_=sp[:, P : P + 8])
-        nbt = const.tile([P, 1], F32, name="nbt")
-        nc.vector.tensor_scalar_mul(nbt[:], bcol[:, 2:3], -1.0)
-
-        sg = const.tile([P, 2], F32, name="sg")
-        nc.scalar.activation(out=sg[:], in_=bcol[:, 3:5], func=ACT.Sigmoid, scale=-1.0)
+            if b == 3:
+                nc.sync.dma_start(out=brow2[0:2, :], in_=b_gd.rearrange("(a k) -> a k", a=2))
+                nc.sync.dma_start(out=brow2[2:3, :], in_=gleak.rearrange("(a k) -> a k", a=1))
+                nc.sync.dma_start(out=brow2[3:4, :], in_=cm.rearrange("(a k) -> a k", a=1))
 
         tau = [keep.tile([P, 4 * CH], F32, name="tau%d" % b) for b in range(NB)]
         codes = [
@@ -115,10 +116,12 @@ def tile_ltcattentioncell_t_kernel(
         ]
 
         hTs = {}
-        zrings = [(psx, "x")] * 4 + [(psb, "b")] * 2
+        zrings = [(psx, "x")] * 4
+        hrings = [(psa, "a"), (psa, "a"), (psb, "b")]
 
         def h_transposes(u):
-            hp = psa.tile([P, 2 * CH], BF16, name="hp", tag="a")
+            ring = hrings[u % len(hrings)]
+            hp = ring[0].tile([P, 2 * CH], BF16, name="hp", tag=ring[1])
             src = htiles[u // 2]
             for j in range(GS):
                 nc.tensor.transpose(
@@ -126,7 +129,7 @@ def tile_ltcattentioncell_t_kernel(
                     in_=src[:, (u % 2) * GS + j, :],
                     identity=identb[:],
                 )
-            hT = small.tile([P, 2 * CH], BF16, name="hT", tag="hT")
+            hT = htp.tile([P, 2 * CH], BF16, name="hT")
             nc.vector.tensor_copy(out=hT[:], in_=hp[:])
             hTs[u] = hT
 
@@ -148,18 +151,7 @@ def tile_ltcattentioncell_t_kernel(
                 scale=-1.0,
             )
 
-        h_transposes(0)
-        h_transposes(1)
-        kap = const.tile([P, 1], F32, name="kap")
-        nc.vector.tensor_tensor(out=kap[:], in0=sg[:, 0:1], in1=sg[:, 1:2], op=ALU.mult)
-        nc.vector.tensor_scalar_mul(kap[:], kap[:], math.exp(-1e-6))
-        for u in range(NG):
-            tau_chunk(2 * u)
-            tau_chunk(2 * u + 1)
-            if u + 2 < NG:
-                h_transposes(u + 2)
-
-        wraw = const.tile([P, 2, K], BF16, name="wraw")
+        wraw = mid.tile([P, 2, K], BF16, name="wraw", tag="mid", align_bytes=64)
         nc.sync.dma_start(out=wraw[:], in_=W_gd.rearrange("(a p) k -> p a k", p=P))
         combs = {}
 
@@ -168,14 +160,17 @@ def tile_ltcattentioncell_t_kernel(
             sl = slice(g * GS, (g + 1) * GS)
             nc.sync.dma_start(out=cb[:, :, 0:IN_DIM], in_=xv[:, sl, :])
             nc.sync.dma_start(out=cb[:, :, IN_DIM + HID : K], in_=cv[:, sl, :])
+            combs[g] = cb
             if g % H_MOD < H_DMA:
                 nc.sync.dma_start(out=cb[:, :, IN_DIM : IN_DIM + HID], in_=hv[:, sl, :])
-            else:
-                nc.vector.tensor_copy(
-                    out=cb[:, :, IN_DIM : IN_DIM + HID],
-                    in_=htiles[g // 2][:, (g % 2) * GS : (g % 2 + 1) * GS, :],
-                )
-            combs[g] = cb
+            elif g >= NBIG:
+                copy_h(g)
+
+        def copy_h(g):
+            nc.vector.tensor_copy(
+                out=combs[g][:, :, IN_DIM : IN_DIM + HID],
+                in_=htiles[g // 2][:, (g % 2) * GS : (g % 2 + 1) * GS, :],
+            )
 
         for g in range(NBIG):
             load_comb(g)
@@ -202,7 +197,7 @@ def tile_ltcattentioncell_t_kernel(
         def word_transposes(src, s0):
             words = src[:].bitcast(F32).rearrange("p s (w u) -> p s u w", u=2)
             ring = rings[ring_pos[0] % len(rings)]
-            if ring_pos[0] >= EARLY[0] - 3:
+            if not F_EARLY < ring_pos[0] < EARLY[0] - 2:
                 ring = rings[4 + ring_pos[0] % 4]
             ring_pos[0] += 1
             xt = ring[0].tile([P, 2, 2 * P], F32, name="xt", tag=ring[1])
@@ -228,11 +223,76 @@ def tile_ltcattentioncell_t_kernel(
                     in_=xt[:].rearrange("p u c -> p c u"),
                 )
 
-        wgrp = const.tile([P, 4 * 2 * HID], BF16, name="wgrp", align_bytes=64)
+        wgrp = mid.tile([P, 4 * 2 * HID], BF16, name="wgrp", tag="mid", align_bytes=64)
         wcodes = const.tile([P, 2 * HID], U32, name="wcodes", align_bytes=64)
         wplane = const.tile([P, 2 * HID], U8, name="wplane", align_bytes=64)
-        regroup(word_transposes(wraw, 0), wgrp, 0, False)
-        ring_pos[0] = 0
+
+        groupeds = {}
+
+        def quantise(c):
+            nc.vector.quantize_mx(
+                out=codes[c][:].bitcast(FP8X4), scales=planes[c][:], in_=groupeds[c][:]
+            )
+
+        def front_step(k):
+            c, half = divmod(k, 2)
+            if half == 0:
+                groupeds[c] = mid.tile([P, 4 * CH], BF16, name="grouped", tag="mid", align_bytes=64)
+            xt = word_transposes(combs[c // 2], (c % 2) * 4 + half * 2)
+            regroup(xt, groupeds[c], half, k % S_EVERY == S_PHASE and S_FROM <= k < JOB_END)
+
+        hp = psa.tile([P, 2 * CH], BF16, name="hp", tag="a")
+        hTs[0] = htp.tile([P, 2 * CH], BF16, name="hT")
+        sp = psb.tile([P, 2 * P], BF16, name="sp", tag="b")
+        wtT = const.tile([P, HID], BF16, name="wtT")
+        bcol = const.tile([P, 8], F32, name="bcol")
+        nbt = const.tile([P, 1], F32, name="nbt")
+        def first_half(half):
+            cols = slice(half * CH, (half + 1) * CH)
+            for j in range(4 * half, 4 * half + 4):
+                nc.tensor.transpose(
+                    out=hp[:, j * P : (j + 1) * P], in_=htiles[0][:, j, :], identity=identb[:]
+                )
+            nc.vector.tensor_copy(out=hTs[0][:, cols], in_=hp[:, cols])
+
+        first_half(0)
+        nc.tensor.transpose(out=sp[:, 0:P], in_=wtau[:], identity=identb[:])
+        nc.tensor.transpose(out=sp[:, P : 2 * P], in_=brow[:], identity=identb[:])
+        nc.vector.tensor_copy(out=wtT[:], in_=sp[:, 0:P])
+        nc.vector.tensor_scalar_mul(nbt[:], sp[:, P : P + 1], -1.0)
+        first_half(1)
+        tau_chunk(0)
+        h_transposes(1)
+        tau_chunk(1)
+        h_transposes(2)
+
+        sg = const.tile([P, 2], F32, name="sg")
+        kap = const.tile([P, 1], F32, name="kap")
+        for u in range(NG):
+            if u > 0:
+                tau_chunk(2 * u)
+                tau_chunk(2 * u + 1)
+            if u + 3 < NG:
+                h_transposes(u + 3)
+            if u in (9, 11):
+                copy_h(1 if u == 9 else 3)
+            if u == W_AT:
+                regroup(word_transposes(wraw, 0), wgrp, 0, False)
+            if u == W_AT + 1:
+                nc.vector.quantize_mx(out=wcodes[:].bitcast(FP8X4), scales=wplane[:], in_=wgrp[:])
+            if u in F_AT:
+                for k in F_AT[u]:
+                    front_step(k)
+            if u == 6:
+                sp2 = psb.tile([P, P], BF16, name="sp2", tag="b")
+                nc.tensor.transpose(out=sp2[:], in_=brow2[:], identity=identb[:])
+                nc.vector.tensor_copy(out=bcol[:], in_=sp2[:, 0:8])
+            if u == 8:
+                nc.scalar.activation(out=sg[:], in_=bcol[:, 2:4], func=ACT.Sigmoid, scale=-1.0)
+            if u == 10:
+                nc.vector.tensor_tensor(out=kap[:], in0=sg[:, 0:1], in1=sg[:, 1:2], op=ALU.mult)
+            if u == 11:
+                nc.vector.tensor_scalar_mul(kap[:], kap[:], math.exp(-1e-6))
 
         sts = {}
         outs = {}
@@ -309,7 +369,7 @@ def tile_ltcattentioncell_t_kernel(
             nc.vector.tensor_tensor(out=nums[c][:], in0=ats[c][:], in1=hn, op=ALU.subtract)
 
         def once(c):
-            first = small.tile([P, CH], F32, name="first", tag="hT")
+            first = small.tile([P, CH], F32, name="first", tag="first")
             nc.vector.tensor_tensor(out=first[:], in0=rts[c][:], in1=nums[c][:], op=ALU.mult)
             nums[c] = first
 
@@ -365,28 +425,16 @@ def tile_ltcattentioncell_t_kernel(
             square(2 * u)
             square(2 * u + 1)
 
-        groupeds = {}
-
-        def quantise(c):
-            nc.vector.quantize_mx(
-                out=codes[c][:].bitcast(FP8X4), scales=planes[c][:], in_=groupeds[c][:]
-            )
-
-        for c in range(NCH):
-            groupeds[c] = mid.tile([P, 4 * CH], BF16, name="grouped", tag="mid", align_bytes=64)
-            for half in range(2):
-                k = 2 * c + half
-                if k in jobs_at:
-                    jobs_at[k][0](jobs_at[k][1])
-                xt = word_transposes(combs[c // 2], (c % 2) * 4 + half * 2)
-                regroup(xt, groupeds[c], half, k % S_EVERY == S_PHASE and S_FROM <= k < JOB_END)
-                if k in EARLY:
-                    start_pair(EARLY.index(k), False)
-            if c == 0:
-                nc.vector.quantize_mx(
-                    out=wcodes[:].bitcast(FP8X4), scales=wplane[:], in_=wgrp[:]
-                )
-            if c % 2 == 1:
+        first_steps = sum([len(f) for f in F_AT.values()])
+        for k in range(2 * NCH):
+            if k in jobs_at:
+                jobs_at[k][0](jobs_at[k][1])
+            if k >= first_steps:
+                front_step(k)
+            if k in EARLY:
+                start_pair(EARLY.index(k), False)
+            if k % 4 == 3:
+                c = k // 2
                 quantise(c - 1)
                 quantise(c)
                 sq = c - 2 * G_FIRST
@@ -399,8 +447,9 @@ def tile_ltcattentioncell_t_kernel(
                 if c // 2 == P_AT:
                     product(0)
                     product(1)
-            if c % 2 == 1 and c // 2 + NBIG < NG:
-                load_comb(c // 2 + NBIG)
+                if c // 2 + NBIG < NG:
+                    load_comb(c // 2 + NBIG)
+
         for c in range(2 if P_AT < NG else 0, 2 * len(EARLY)):
             product(c)
         started = len(EARLY)

@@ -22,7 +22,7 @@ GS = 8
 NG = SLOTS // GS
 HS = 16
 NB = SLOTS // HS
-PAIR_PROD = False
+PAIR_PROD = range(3, 14)
 HB = 1024
 S_EVERY = 5
 S_PHASE = 2
@@ -71,22 +71,22 @@ def tile_ltcattentioncell_t_kernel(
         psb = ctx.enter_context(tc.psum_pool(name="psb", bufs=2))
         ctx.enter_context(tc.manual_schedule())
 
-        wbf = const.tile([P, CH], BF16, name="wbf")
+        brow = const.tile([P, P], BF16, name="brow")
+        nc.vector.memset(brow[:], 0.0)
+        wbf = const.tile([P, 2 * P], BF16, name="wbf")
         nc.vector.memset(wbf[:], 0.0)
         identb = const.tile([P, P], BF16, name="identb")
         identf = const.tile([P, P], F32, name="identf")
         make_identity(nc, identb[:])
         make_identity(nc, identf[:])
-        brow = const.tile([P, P], BF16, name="brow")
-        nc.vector.memset(brow[:], 0.0)
+        warm = const.tile([P, 1], F32, name="warm")
+        nc.vector.memset(warm[:], 0.0)
         brow2 = const.tile([P, P], BF16, name="brow2")
         nc.vector.memset(brow2[:], 0.0)
 
         for i in range(WARM):
-            wps = psx.tile([P, CH], F32, name="wps", tag="x")
+            wps = psx.tile([P, 2 * P], F32, name="wps", tag="x")
             nc.tensor.matmul(out=wps[:], lhsT=wbf[:, 0:P], rhs=wbf[:], start=True, stop=True)
-        warm = const.tile([P, 1], F32, name="warm")
-        nc.vector.memset(warm[:], 0.0)
 
         htiles = [keep.tile([P, HS, HID], BF16, name="ht%d" % b) for b in range(NB)]
 
@@ -96,7 +96,7 @@ def tile_ltcattentioncell_t_kernel(
         load_h(0, 0, GS // 2)
         wtau = const.tile([P, HID], BF16, name="wtau")
         nc.scalar.dma_start(out=wtau[:], in_=W_tau)
-        nc.scalar.dma_start(out=brow[0:1, :], in_=b_tau.rearrange("(a k) -> a k", a=1))
+        nc.sync.dma_start(out=brow[0:1, :], in_=b_tau.rearrange("(a k) -> a k", a=1))
         nc.scalar.activation(out=warm[:], in_=warm[:], func=ACT.Sigmoid)
         load_h(0, GS // 2, GS)
         load_h(0, GS, HS)
@@ -321,7 +321,7 @@ def tile_ltcattentioncell_t_kernel(
 
         def product(c):
             st = sts[c // 2]
-            if PAIR_PROD:
+            if c // 2 in PAIR_PROD:
                 if c % 2 == 1:
                     nc.gpsimd.tensor_tensor(
                         out=st[:, 0:2, :], in0=st[:, 0:2, :], in1=st[:, 2:4, :], op=ALU.mult

@@ -24,15 +24,20 @@ HS = 16
 NB = SLOTS // HS
 PAIR_PROD = range(3, 14)
 HB = 1024
-S_EVERY = 5
-S_PHASE = 2
+S_EVERY = 8
+S_PHASE = 0
 JOB_END = 56
-S_FROM = 20
+S_FROM = 14
 V_PROD = ()
 LAG2 = 2
 LAG_END = 11
+LATE_SQ = ()
+LATE_AT = 13
+READY = (28, 29, 30, 31)
+R_STEP = 40
+R_EVERY = 3
 P_AT = 14
-EARLY = (56, 59, 62)
+EARLY = (57, 60, 62)
 SQ = "SDSDSDSD"
 TAIL_S = 4
 G_L = 9
@@ -44,7 +49,7 @@ H_DMA = 1
 WARM = 4
 W_AT = 13
 F_AT = {14: (0, 1), 15: ()}
-F_EARLY = 3
+F_EARLY = 2
 NBIG = 4
 
 FLOPS = 2 * B * K * 2 * HID + 2 * B * HID * HID
@@ -83,6 +88,9 @@ def tile_ltcattentioncell_t_kernel(
         nc.vector.memset(warm[:], 0.0)
         brow2 = const.tile([P, P], BF16, name="brow2")
         nc.vector.memset(brow2[:], 0.0)
+
+        negb = const.tile([P, P], BF16, name="negb")
+        nc.vector.tensor_scalar_mul(negb[:], identb[:], -1.0)
 
         for i in range(WARM):
             wps = psx.tile([P, 2 * P], F32, name="wps", tag="x")
@@ -182,6 +190,19 @@ def tile_ltcattentioncell_t_kernel(
         def job_ln(j):
             nc.scalar.activation(out=tau_part(j), in_=tau_part(j), func=ACT.Ln, scale=kap[:, 0:1])
 
+        def tau_chunk_view(c):
+            return tau[c // 4][:, (c % 4) * CH : (c % 4 + 1) * CH]
+
+        def job_ready(c):
+            r = tau_chunk_view(c)
+            ring = next_ring()
+            rq = ring[0].tile([P, CH], F32, name="rq", tag=ring[1])
+            for j in range(4):
+                nc.tensor.transpose(
+                    out=rq[:, j * P : (j + 1) * P], in_=r[:, j * P : (j + 1) * P], identity=identf[:]
+                )
+            nc.scalar.activation(out=r, in_=rq[:], func=ACT.Square)
+
         def job_rs(j):
             nc.scalar.activation(out=tau_part(j), in_=tau_part(j), func=ACT.Abs_reciprocal_sqrt)
 
@@ -193,13 +214,19 @@ def tile_ltcattentioncell_t_kernel(
 
         rings = [(psx, "x")] * 4 + [(psa, "a")] * 2 + [(psb, "b")] * 2
         ring_pos = [0]
+        step = [0]
+
+        def next_ring():
+            ring = rings[ring_pos[0] % len(rings)]
+            if step[0] < F_EARLY or step[0] >= EARLY[0] - 3:
+                ring = rings[4 + ring_pos[0] % 4]
+            ring_pos[0] += 1
+            return ring
+
 
         def word_transposes(src, s0):
             words = src[:].bitcast(F32).rearrange("p s (w u) -> p s u w", u=2)
-            ring = rings[ring_pos[0] % len(rings)]
-            if not F_EARLY < ring_pos[0] < EARLY[0] - 2:
-                ring = rings[4 + ring_pos[0] % 4]
-            ring_pos[0] += 1
+            ring = next_ring()
             xt = ring[0].tile([P, 2, 2 * P], F32, name="xt", tag=ring[1])
             for jj in range(2):
                 for u in range(2):
@@ -236,6 +263,7 @@ def tile_ltcattentioncell_t_kernel(
 
         def front_step(k):
             c, half = divmod(k, 2)
+            step[0] = k
             if half == 0:
                 groupeds[c] = mid.tile([P, 4 * CH], BF16, name="grouped", tag="mid", align_bytes=64)
             xt = word_transposes(combs[c // 2], (c % 2) * 4 + half * 2)
@@ -332,6 +360,8 @@ def tile_ltcattentioncell_t_kernel(
                 eng.tensor_tensor(out=a, in0=a, in1=st[:, 2 + c % 2, :], op=ALU.mult)
 
         def who(c):
+            if c in READY:
+                return "R"
             kind = "S" if c >= NCH - TAIL_S else SQ[c % 8]
             return "S" if kind == "D" and c // 2 + G_FIRST >= P_AT else kind
 
@@ -355,13 +385,34 @@ def tile_ltcattentioncell_t_kernel(
 
         def back_a(c):
             a = sts[c // 2][:, c % 2, :]
-            ats[c] = psa.tile([P, CH], F32, name="at", tag="a")
-            for j in range(4):
-                nc.tensor.transpose(
-                    out=ats[c][:, j * P : (j + 1) * P],
-                    in_=a[:, j * P : (j + 1) * P],
-                    identity=identf[:],
+            if who(c) == "R" and c % 2 == 0:
+                ats[c] = psb.tile([P, CH], F32, name="at", tag="b")
+            else:
+                ats[c] = psa.tile([P, CH], F32, name="at", tag="a")
+            if who(c) == "R":
+                nc.tensor.matmul(
+                    out=ats[c][:],
+                    lhsT=negb[:],
+                    rhs=htiles[c // 4][:, (c % 4) * 4 : (c % 4 + 1) * 4, :].rearrange("p s k -> p (s k)"),
+                    start=True,
+                    stop=False,
                 )
+            for j in range(4):
+                if who(c) == "R":
+                    nc.tensor.matmul(
+                        out=ats[c][:, j * P : (j + 1) * P],
+                        lhsT=a[:, j * P : (j + 1) * P],
+                        rhs=identf[:],
+                        is_transpose=True,
+                        start=False,
+                        stop=(j == 3),
+                    )
+                else:
+                    nc.tensor.transpose(
+                        out=ats[c][:, j * P : (j + 1) * P],
+                        in_=a[:, j * P : (j + 1) * P],
+                        identity=identf[:],
+                    )
 
         def numerator(c):
             nums[c] = small.tile([P, CH], F32, name="num", tag="num")
@@ -379,8 +430,8 @@ def tile_ltcattentioncell_t_kernel(
             o = outs[c // 2]
             nc.vector.tensor_tensor(
                 out=o[:, (c % 2) * CH : (c % 2 + 1) * CH],
-                in0=rts[c][:],
-                in1=nums[c][:],
+                in0=(ats[c][:] if who(c) == "R" else rts[c][:]),
+                in1=(tau_chunk_view(c) if who(c) == "R" else nums[c][:]),
                 op=ALU.mult,
             )
             if alone:
@@ -393,13 +444,14 @@ def tile_ltcattentioncell_t_kernel(
             c0, c1 = 2 * v, 2 * v + 1
             back_a(c1)
             back_a(c0)
-            back_r(c1)
-            back_r(c0)
+            plain = [c for c in (c1, c0) if who(c) != "R"]
+            for c in plain:
+                back_r(c)
             for c in (2 * v + 2, 2 * v + 3):
                 if c in V_PROD:
                     product(c)
-            numerator(c1)
-            numerator(c0)
+            for c in plain:
+                numerator(c)
             twice = [c for c in (c1, c0) if who(c) == "V"]
             for c in twice:
                 once(c)
@@ -422,13 +474,19 @@ def tile_ltcattentioncell_t_kernel(
             for c in (2 * u, 2 * u + 1):
                 if products and c not in V_PROD:
                     product(c)
-            square(2 * u)
-            square(2 * u + 1)
+            for c in (2 * u, 2 * u + 1):
+                if c not in LATE_SQ:
+                    square(c)
+            for c in LATE_SQ:
+                if u == LATE_AT:
+                    square(c)
 
         first_steps = sum([len(f) for f in F_AT.values()])
         for k in range(2 * NCH):
             if k in jobs_at:
                 jobs_at[k][0](jobs_at[k][1])
+            if k >= R_STEP and (k - R_STEP) % R_EVERY == 0 and (k - R_STEP) // R_EVERY < len(READY):
+                job_ready(READY[(k - R_STEP) // R_EVERY])
             if k >= first_steps:
                 front_step(k)
             if k in EARLY:

@@ -31,8 +31,7 @@ S_FROM = 14
 V_PROD = ()
 LAG2 = 2
 LAG_END = 11
-LATE_SQ = ()
-LATE_AT = 13
+MORE = 192
 READY = (28, 29, 30, 31)
 R_STEP = 40
 R_EVERY = 3
@@ -47,6 +46,7 @@ LAG = 3
 H_MOD = 2
 H_DMA = 1
 WARM = 4
+H_AT = (5, 7, 9, 11)
 W_AT = 13
 F_AT = {14: (0, 1), 15: ()}
 F_EARLY = 2
@@ -169,7 +169,7 @@ def tile_ltcattentioncell_t_kernel(
             nc.sync.dma_start(out=cb[:, :, 0:IN_DIM], in_=xv[:, sl, :])
             nc.sync.dma_start(out=cb[:, :, IN_DIM + HID : K], in_=cv[:, sl, :])
             combs[g] = cb
-            if g % H_MOD < H_DMA:
+            if g >= NBIG and g % H_MOD < H_DMA:
                 nc.sync.dma_start(out=cb[:, :, IN_DIM : IN_DIM + HID], in_=hv[:, sl, :])
             elif g >= NBIG:
                 copy_h(g)
@@ -302,8 +302,8 @@ def tile_ltcattentioncell_t_kernel(
                 tau_chunk(2 * u + 1)
             if u + 3 < NG:
                 h_transposes(u + 3)
-            if u in (9, 11):
-                copy_h(1 if u == 9 else 3)
+            if u in H_AT:
+                copy_h(H_AT.index(u))
             if u == W_AT:
                 regroup(word_transposes(wraw, 0), wgrp, 0, False)
             if u == W_AT + 1:
@@ -366,9 +366,13 @@ def tile_ltcattentioncell_t_kernel(
             return "S" if kind == "D" and c // 2 + G_FIRST >= P_AT else kind
 
         def square(c):
-            r = tau[c // 4][:, (c % 4) * CH : (c % 4 + 1) * CH]
             if who(c) == "S":
+                n = CH - (more(c + 1) if c % 2 == 0 and who(c + 1) == "D" else 0)
+                r = tau[c // 4][:, (c % 4) * CH : (c % 4) * CH + n]
                 nc.scalar.activation(out=r, in_=r, func=ACT.Square)
+
+        def more(c):
+            return MORE if c // 2 % 2 == 1 else 0
 
         rts = {}
         ats = {}
@@ -474,12 +478,8 @@ def tile_ltcattentioncell_t_kernel(
             for c in (2 * u, 2 * u + 1):
                 if products and c not in V_PROD:
                     product(c)
-            for c in (2 * u, 2 * u + 1):
-                if c not in LATE_SQ:
-                    square(c)
-            for c in LATE_SQ:
-                if u == LATE_AT:
-                    square(c)
+            square(2 * u)
+            square(2 * u + 1)
 
         first_steps = sum([len(f) for f in F_AT.values()])
         for k in range(2 * NCH):
@@ -500,7 +500,7 @@ def tile_ltcattentioncell_t_kernel(
                     tick = small.tile([P, 1], U32, name="tick", tag="tick")
                     nc.gpsimd.tensor_copy(out=tick[:], in_=codes[c][:, 0:1])
                 if sq >= 0 and who(sq) == "D":
-                    r = tau[sq // 4][:, (sq % 4) * CH : (sq % 4 + 1) * CH]
+                    r = tau[sq // 4][:, (sq % 4) * CH - more(sq) : (sq % 4 + 1) * CH]
                     nc.gpsimd.tensor_tensor(out=r, in0=r, in1=r, op=ALU.mult)
                 if c // 2 == P_AT:
                     product(0)

@@ -32,11 +32,12 @@ V_PROD = ()
 LAG2 = 2
 LAG_END = 11
 MORE = 192
-READY = (28, 29, 30, 31)
+ALONE = 13
+READY = (20, 28, 29, 30, 31)
 R_STEP = 40
 R_EVERY = 3
 P_AT = 14
-EARLY = (57, 60, 62)
+EARLY = (56, 60, 63)
 SQ = "SDSDSDSD"
 TAIL_S = 4
 G_L = 9
@@ -372,7 +373,7 @@ def tile_ltcattentioncell_t_kernel(
                 nc.scalar.activation(out=r, in_=r, func=ACT.Square)
 
         def more(c):
-            return MORE if c // 2 % 2 == 1 else 0
+            return MORE if c // 2 % 2 == 1 and who(c - 1) == "S" else 0
 
         rts = {}
         ats = {}
@@ -445,10 +446,11 @@ def tile_ltcattentioncell_t_kernel(
                 )
 
         def finish_pair(v):
-            c0, c1 = 2 * v, 2 * v + 1
-            back_a(c1)
-            back_a(c0)
+            c0, c1 = (2 * v, 2 * v + 1) if v < NG - 1 else (2 * v + 1, 2 * v)
             plain = [c for c in (c1, c0) if who(c) != "R"]
+            done = [c for c in (c1, c0) if who(c) == "R"]
+            for c in (c1, c0):
+                back_a(c)
             for c in plain:
                 back_r(c)
             for c in (2 * v + 2, 2 * v + 3):
@@ -456,15 +458,17 @@ def tile_ltcattentioncell_t_kernel(
                     product(c)
             for c in plain:
                 numerator(c)
+            for c in done:
+                result(c, v >= ALONE)
             twice = [c for c in (c1, c0) if who(c) == "V"]
             for c in twice:
                 once(c)
-            for c in (c1, c0):
+            for c in plain:
                 if c not in twice:
-                    result(c, v == NG - 1)
+                    result(c, v >= ALONE)
             for c in twice:
-                result(c, v == NG - 1)
-            if v < NG - 1:
+                result(c, v >= ALONE)
+            if v < ALONE:
                 nc.sync.dma_start(
                     out=ov[:, v * GS : (v + 1) * GS, :],
                     in_=outs[v][:].rearrange("p (s f) -> p s f", f=HID),

@@ -25,13 +25,14 @@ NB = SLOTS // HS
 PAIR_PROD = range(3, 14)
 HB = 1024
 S_EVERY = 8
-S_PHASE = 0
+S_PHASE = 1
 JOB_END = 56
 S_FROM = 14
 V_PROD = ()
 LAG2 = 2
 LAG_END = 11
 MORE = 192
+Q_AT = 0
 ALONE = 13
 READY = (20, 28, 29, 30, 31)
 R_STEP = 40
@@ -69,7 +70,7 @@ def tile_ltcattentioncell_t_kernel(
         const = ctx.enter_context(tc.tile_pool(name="const", bufs=1))
         keep = ctx.enter_context(tc.tile_pool(name="keep", bufs=1))
         big = ctx.enter_context(tc.tile_pool(name="big", bufs=NBIG))
-        mid = ctx.enter_context(tc.tile_pool(name="mid", bufs=3))
+        mid = ctx.enter_context(tc.tile_pool(name="mid", bufs=2))
         small = ctx.enter_context(tc.tile_pool(name="small", bufs=2))
         htp = ctx.enter_context(tc.tile_pool(name="htp", bufs=3))
         psx = ctx.enter_context(tc.psum_pool(name="psx", bufs=4))
@@ -118,10 +119,10 @@ def tile_ltcattentioncell_t_kernel(
 
         tau = [keep.tile([P, 4 * CH], F32, name="tau%d" % b) for b in range(NB)]
         codes = [
-            keep.tile([P, CH], U32, name="codes%d" % c, align_bytes=64) for c in range(NCH)
+            keep.tile([P, 2 * CH], U32, name="codes%d" % g, align_bytes=64) for g in range(NG)
         ]
         planes = [
-            keep.tile([P, CH], U8, name="plane%d" % c, align_bytes=64) for c in range(NCH)
+            keep.tile([P, 2 * CH], U8, name="plane%d" % g, align_bytes=64) for g in range(NG)
         ]
 
         hTs = {}
@@ -257,18 +258,18 @@ def tile_ltcattentioncell_t_kernel(
 
         groupeds = {}
 
-        def quantise(c):
+        def quantise(g):
             nc.vector.quantize_mx(
-                out=codes[c][:].bitcast(FP8X4), scales=planes[c][:], in_=groupeds[c][:]
+                out=codes[g][:].bitcast(FP8X4), scales=planes[g][:], in_=groupeds[g][:]
             )
 
         def front_step(k):
-            c, half = divmod(k, 2)
+            g, part = divmod(k, 4)
             step[0] = k
-            if half == 0:
-                groupeds[c] = mid.tile([P, 4 * CH], BF16, name="grouped", tag="mid", align_bytes=64)
-            xt = word_transposes(combs[c // 2], (c % 2) * 4 + half * 2)
-            regroup(xt, groupeds[c], half, k % S_EVERY == S_PHASE and S_FROM <= k < JOB_END)
+            if part == 0:
+                groupeds[g] = mid.tile([P, 8 * CH], BF16, name="grouped", tag="mid", align_bytes=64)
+            xt = word_transposes(combs[g], part * 2)
+            regroup(xt, groupeds[g], part, k % S_EVERY == S_PHASE and S_FROM <= k < JOB_END)
 
         hp = psa.tile([P, 2 * CH], BF16, name="hp", tag="a")
         hTs[0] = htp.tile([P, 2 * CH], BF16, name="hT")
@@ -330,14 +331,15 @@ def tile_ltcattentioncell_t_kernel(
             if c % 2 == 0:
                 sts[c // 2] = big.tile([P, 4, CH], F32, name="st", tag="big")
             st = sts[c // 2]
+            cols = slice((c % 2) * CH, (c % 2 + 1) * CH)
             for i in range(2):
                 g = psx.tile([P, CH], F32, name="g", tag="x")
                 nc.tensor.matmul_mx(
                     out=g[:],
                     lhsT=wcodes[:, i * HID : (i + 1) * HID].bitcast(FP8X4),
                     lhsT_scale=wplane[:, i * HID : (i + 1) * HID],
-                    rhs=codes[c][:].bitcast(FP8X4),
-                    rhs_scale=planes[c][:],
+                    rhs=codes[c // 2][:, cols].bitcast(FP8X4),
+                    rhs_scale=planes[c // 2][:, cols],
                     start=True,
                     stop=True,
                 )
@@ -430,11 +432,11 @@ def tile_ltcattentioncell_t_kernel(
             nums[c] = first
 
         def result(c, alone):
-            if c // 2 not in outs:
-                outs[c // 2] = mid.tile([P, 2 * CH], F32, name="o", tag="mid", align_bytes=64)
-            o = outs[c // 2]
+            if c // 4 not in outs:
+                outs[c // 4] = mid.tile([P, 4 * CH], F32, name="o", tag="mid", align_bytes=64)
+            o = outs[c // 4]
             nc.vector.tensor_tensor(
-                out=o[:, (c % 2) * CH : (c % 2 + 1) * CH],
+                out=o[:, (c % 4) * CH : (c % 4 + 1) * CH],
                 in0=(ats[c][:] if who(c) == "R" else rts[c][:]),
                 in1=(tau_chunk_view(c) if who(c) == "R" else nums[c][:]),
                 op=ALU.mult,
@@ -442,7 +444,7 @@ def tile_ltcattentioncell_t_kernel(
             if alone:
                 nc.sync.dma_start(
                     out=ov[:, c * 4 : (c + 1) * 4, :],
-                    in_=o[:, (c % 2) * CH : (c % 2 + 1) * CH].rearrange("p (s f) -> p s f", f=HID),
+                    in_=o[:, (c % 4) * CH : (c % 4 + 1) * CH].rearrange("p (s f) -> p s f", f=HID),
                 )
 
         def finish_pair(v):
@@ -471,7 +473,9 @@ def tile_ltcattentioncell_t_kernel(
             if v < ALONE:
                 nc.sync.dma_start(
                     out=ov[:, v * GS : (v + 1) * GS, :],
-                    in_=outs[v][:].rearrange("p (s f) -> p s f", f=HID),
+                    in_=outs[v // 2][:, (v % 2) * 2 * CH : (v % 2 + 1) * 2 * CH].rearrange(
+                        "p (s f) -> p s f", f=HID
+                    ),
                 )
 
         nums = {}
@@ -486,6 +490,21 @@ def tile_ltcattentioncell_t_kernel(
             square(2 * u + 1)
 
         first_steps = sum([len(f) for f in F_AT.values()])
+        def after_quantise(g):
+            quantise(g)
+            if g + NBIG < NG:
+                load_comb(g + NBIG)
+            if g >= G_FIRST:
+                tick = small.tile([P, 1], U32, name="tick", tag="tick")
+                nc.gpsimd.tensor_copy(out=tick[:], in_=codes[g][:, 0:1])
+            sq = 2 * (g - G_FIRST) + 1
+            if sq >= 0 and who(sq) == "D":
+                r = tau[sq // 4][:, (sq % 4) * CH - more(sq) : (sq % 4 + 1) * CH]
+                nc.gpsimd.tensor_tensor(out=r, in0=r, in1=r, op=ALU.mult)
+            if g == P_AT:
+                product(0)
+                product(1)
+
         for k in range(2 * NCH):
             if k in jobs_at:
                 jobs_at[k][0](jobs_at[k][1])
@@ -495,22 +514,9 @@ def tile_ltcattentioncell_t_kernel(
                 front_step(k)
             if k in EARLY:
                 start_pair(EARLY.index(k), False)
-            if k % 4 == 3:
-                c = k // 2
-                quantise(c - 1)
-                quantise(c)
-                sq = c - 2 * G_FIRST
-                if c // 2 >= G_FIRST:
-                    tick = small.tile([P, 1], U32, name="tick", tag="tick")
-                    nc.gpsimd.tensor_copy(out=tick[:], in_=codes[c][:, 0:1])
-                if sq >= 0 and who(sq) == "D":
-                    r = tau[sq // 4][:, (sq % 4) * CH - more(sq) : (sq % 4 + 1) * CH]
-                    nc.gpsimd.tensor_tensor(out=r, in0=r, in1=r, op=ALU.mult)
-                if c // 2 == P_AT:
-                    product(0)
-                    product(1)
-                if c // 2 + NBIG < NG:
-                    load_comb(c // 2 + NBIG)
+            if k % 4 == Q_AT and k > Q_AT:
+                after_quantise((k - Q_AT) // 4 - 1)
+        after_quantise(NG - 1)
 
         for c in range(2 if P_AT < NG else 0, 2 * len(EARLY)):
             product(c)

@@ -31,12 +31,12 @@ S_FROM = 14
 V_PROD = ()
 LAG2 = 2
 LAG_END = 11
-MORE = 192
+MORE = 224
 Q_AT = 0
 ALONE = 13
-READY = (20, 28, 29, 30, 31)
-R_STEP = 40
-R_EVERY = 3
+READY = (20, 26, 28, 29, 30, 31)
+R_STEP = 42
+R_EVERY = 2
 P_AT = 14
 EARLY = (56, 60, 63)
 SQ = "SDSDSDSD"

import math
from contextlib import ExitStack

import concourse.mybir as mybir
from concourse.masks import make_identity

F32 = mybir.dt.float32
BF16 = mybir.dt.bfloat16
U32 = mybir.dt.uint32
U8 = mybir.dt.uint8
FP8X4 = mybir.dt.float8_e4m3fn_x4
ACT = mybir.ActivationFunctionType
ALU = mybir.AluOpType

P = 128
B, IN_DIM, HID, ATT = 16384, 128, 128, 256
K = IN_DIM + HID + ATT
SLOTS = B // P
CH = 512
NCH = B // CH
GS = 8
NG = SLOTS // GS
HS = 16
NB = SLOTS // HS
PAIR_PROD = range(3, 14)
HB = 1024
S_EVERY = 8
S_PHASE = 1
JOB_END = 56
S_FROM = 14
V_PROD = ()
LAG2 = 2
LAG_END = 11
MORE = 224
Q_AT = 0
ALONE = 13
READY = (20, 26, 28, 29, 30, 31)
R_STEP = 42
R_EVERY = 2
P_AT = 14
EARLY = (56, 60, 63)
SQ = "SDSDSDSD"
TAIL_S = 4
G_L = 9
G_FIRST = 1
GW = 512
LAG = 3
H_MOD = 2
H_DMA = 1
WARM = 4
H_AT = (5, 7, 9, 11)
W_AT = 13
F_AT = {14: (0, 1), 15: ()}
F_EARLY = 2
NBIG = 4

FLOPS = 2 * B * K * 2 * HID + 2 * B * HID * HID


def tile_ltcattentioncell_t_kernel(
    tc, t, h_ltc, x_t, context, W_gd, b_gd, W_tau, b_tau, gleak, cm, out
):
    nc = tc.nc
    hv = h_ltc.rearrange("(p s) k -> p s k", s=SLOTS)
    xv = x_t.rearrange("(p s) k -> p s k", s=SLOTS)
    cv = context.rearrange("(p s) k -> p s k", s=SLOTS)
    ov = out.rearrange("(p s) f -> p s f", s=SLOTS)

    with ExitStack() as ctx:
        const = ctx.enter_context(tc.tile_pool(name="const", bufs=1))
        keep = ctx.enter_context(tc.tile_pool(name="keep", bufs=1))
        big = ctx.enter_context(tc.tile_pool(name="big", bufs=NBIG))
        mid = ctx.enter_context(tc.tile_pool(name="mid", bufs=2))
        small = ctx.enter_context(tc.tile_pool(name="small", bufs=2))
        htp = ctx.enter_context(tc.tile_pool(name="htp", bufs=3))
        psx = ctx.enter_context(tc.psum_pool(name="psx", bufs=4))
        psa = ctx.enter_context(tc.psum_pool(name="psa", bufs=2))
        psb = ctx.enter_context(tc.psum_pool(name="psb", bufs=2))
        ctx.enter_context(tc.manual_schedule())

        brow = const.tile([P, P], BF16, name="brow")
        nc.vector.memset(brow[:], 0.0)
        wbf = const.tile([P, 2 * P], BF16, name="wbf")
        nc.vector.memset(wbf[:], 0.0)
        identb = const.tile([P, P], BF16, name="identb")
        identf = const.tile([P, P], F32, name="identf")
        make_identity(nc, identb[:])
        make_identity(nc, identf[:])
        warm = const.tile([P, 1], F32, name="warm")
        nc.vector.memset(warm[:], 0.0)
        brow2 = const.tile([P, P], BF16, name="brow2")
        nc.vector.memset(brow2[:], 0.0)

        negb = const.tile([P, P], BF16, name="negb")
        nc.vector.tensor_scalar_mul(negb[:], identb[:], -1.0)

        for i in range(WARM):
            wps = psx.tile([P, 2 * P], F32, name="wps", tag="x")
            nc.tensor.matmul(out=wps[:], lhsT=wbf[:, 0:P], rhs=wbf[:], start=True, stop=True)

        htiles = [keep.tile([P, HS, HID], BF16, name="ht%d" % b) for b in range(NB)]

        def load_h(b, s0, s1):
            nc.sync.dma_start(out=htiles[b][:, s0:s1, :], in_=hv[:, b * HS + s0 : b * HS + s1, :])

        load_h(0, 0, GS // 2)
        wtau = const.tile([P, HID], BF16, name="wtau")
        nc.scalar.dma_start(out=wtau[:], in_=W_tau)
        nc.sync.dma_start(out=brow[0:1, :], in_=b_tau.rearrange("(a k) -> a k", a=1))
        nc.scalar.activation(out=warm[:], in_=warm[:], func=ACT.Sigmoid)
        load_h(0, GS // 2, GS)
        load_h(0, GS, HS)
        for b in range(1, NB):
            load_h(b, 0, HS)
            if b == 3:
                nc.sync.dma_start(out=brow2[0:2, :], in_=b_gd.rearrange("(a k) -> a k", a=2))
                nc.sync.dma_start(out=brow2[2:3, :], in_=gleak.rearrange("(a k) -> a k", a=1))
                nc.sync.dma_start(out=brow2[3:4, :], in_=cm.rearrange("(a k) -> a k", a=1))

        tau = [keep.tile([P, 4 * CH], F32, name="tau%d" % b) for b in range(NB)]
        codes = [
            keep.tile([P, 2 * CH], U32, name="codes%d" % g, align_bytes=64) for g in range(NG)
        ]
        planes = [
            keep.tile([P, 2 * CH], U8, name="plane%d" % g, align_bytes=64) for g in range(NG)
        ]

        hTs = {}
        zrings = [(psx, "x")] * 4
        hrings = [(psa, "a"), (psa, "a"), (psb, "b")]

        def h_transposes(u):
            ring = hrings[u % len(hrings)]
            hp = ring[0].tile([P, 2 * CH], BF16, name="hp", tag=ring[1])
            src = htiles[u // 2]
            for j in range(GS):
                nc.tensor.transpose(
                    out=hp[:, j * P : (j + 1) * P],
                    in_=src[:, (u % 2) * GS + j, :],
                    identity=identb[:],
                )
            hT = htp.tile([P, 2 * CH], BF16, name="hT")
            nc.vector.tensor_copy(out=hT[:], in_=hp[:])
            hTs[u] = hT

        def tau_chunk(c):
            zr = zrings[c % len(zrings)]
            z = zr[0].tile([P, CH], F32, name="z", tag=zr[1])
            nc.tensor.matmul(
                out=z[:],
                lhsT=wtT[:],
                rhs=hTs[c // 2][:, (c % 2) * CH : (c % 2 + 1) * CH],
                start=True,
                stop=True,
            )
            nc.scalar.activation(
                out=tau[c // 4][:, (c % 4) * CH : (c % 4 + 1) * CH],
                in_=z[:],
                func=ACT.Sigmoid,
                bias=nbt[:, 0:1],
                scale=-1.0,
            )

        wraw = mid.tile([P, 2, K], BF16, name="wraw", tag="mid", align_bytes=64)
        nc.sync.dma_start(out=wraw[:], in_=W_gd.rearrange("(a p) k -> p a k", p=P))
        combs = {}

        def load_comb(g):
            cb = big.tile([P, GS, K], BF16, name="comb", tag="big")
            sl = slice(g * GS, (g + 1) * GS)
            nc.sync.dma_start(out=cb[:, :, 0:IN_DIM], in_=xv[:, sl, :])
            nc.sync.dma_start(out=cb[:, :, IN_DIM + HID : K], in_=cv[:, sl, :])
            combs[g] = cb
            if g >= NBIG and g % H_MOD < H_DMA:
                nc.sync.dma_start(out=cb[:, :, IN_DIM : IN_DIM + HID], in_=hv[:, sl, :])
            elif g >= NBIG:
                copy_h(g)

        def copy_h(g):
            nc.vector.tensor_copy(
                out=combs[g][:, :, IN_DIM : IN_DIM + HID],
                in_=htiles[g // 2][:, (g % 2) * GS : (g % 2 + 1) * GS, :],
            )

        for g in range(NBIG):
            load_comb(g)

        def tau_part(j):
            per = 4 * CH // HB
            return tau[j // per][:, (j % per) * HB : (j % per + 1) * HB]

        def job_ln(j):
            nc.scalar.activation(out=tau_part(j), in_=tau_part(j), func=ACT.Ln, scale=kap[:, 0:1])

        def tau_chunk_view(c):
            return tau[c // 4][:, (c % 4) * CH : (c % 4 + 1) * CH]

        def job_ready(c):
            r = tau_chunk_view(c)
            ring = next_ring()
            rq = ring[0].tile([P, CH], F32, name="rq", tag=ring[1])
            for j in range(4):
                nc.tensor.transpose(
                    out=rq[:, j * P : (j + 1) * P], in_=r[:, j * P : (j + 1) * P], identity=identf[:]
                )
            nc.scalar.activation(out=r, in_=rq[:], func=ACT.Square)

        def job_rs(j):
            nc.scalar.activation(out=tau_part(j), in_=tau_part(j), func=ACT.Abs_reciprocal_sqrt)

        njob = B // HB
        jobs_at = {}
        for j in range(njob):
            jobs_at[(j * JOB_END) // (2 * njob)] = (job_ln, j)
            jobs_at[((j + njob) * JOB_END) // (2 * njob)] = (job_rs, (j + G_L) % njob)

        rings = [(psx, "x")] * 4 + [(psa, "a")] * 2 + [(psb, "b")] * 2
        ring_pos = [0]
        step = [0]

        def next_ring():
            ring = rings[ring_pos[0] % len(rings)]
            if step[0] < F_EARLY or step[0] >= EARLY[0] - 3:
                ring = rings[4 + ring_pos[0] % 4]
            ring_pos[0] += 1
            return ring


        def word_transposes(src, s0):
            words = src[:].bitcast(F32).rearrange("p s (w u) -> p s u w", u=2)
            ring = next_ring()
            xt = ring[0].tile([P, 2, 2 * P], F32, name="xt", tag=ring[1])
            for jj in range(2):
                for u in range(2):
                    nc.tensor.transpose(
                        out=xt[:, u, jj * P : (jj + 1) * P],
                        in_=words[:, s0 + jj, u, :],
                        identity=identf[:],
                    )
            return xt

        def regroup(xt, grouped, half, on_scalar):
            dst = grouped[:].bitcast(F32).rearrange("p (c u) -> p c u", u=2)
            if on_scalar:
                nc.scalar.copy(
                    out=dst[:, half * 2 * P : (half + 1) * 2 * P, :],
                    in_=xt[:].rearrange("p u c -> p c u"),
                )
            else:
                nc.vector.tensor_copy(
                    out=dst[:, half * 2 * P : (half + 1) * 2 * P, :],
                    in_=xt[:].rearrange("p u c -> p c u"),
                )

        wgrp = mid.tile([P, 4 * 2 * HID], BF16, name="wgrp", tag="mid", align_bytes=64)
        wcodes = const.tile([P, 2 * HID], U32, name="wcodes", align_bytes=64)
        wplane = const.tile([P, 2 * HID], U8, name="wplane", align_bytes=64)

        groupeds = {}

        def quantise(g):
            nc.vector.quantize_mx(
                out=codes[g][:].bitcast(FP8X4), scales=planes[g][:], in_=groupeds[g][:]
            )

        def front_step(k):
            g, part = divmod(k, 4)
            step[0] = k
            if part == 0:
                groupeds[g] = mid.tile([P, 8 * CH], BF16, name="grouped", tag="mid", align_bytes=64)
            xt = word_transposes(combs[g], part * 2)
            regroup(xt, groupeds[g], part, k % S_EVERY == S_PHASE and S_FROM <= k < JOB_END)

        hp = psa.tile([P, 2 * CH], BF16, name="hp", tag="a")
        hTs[0] = htp.tile([P, 2 * CH], BF16, name="hT")
        sp = psb.tile([P, 2 * P], BF16, name="sp", tag="b")
        wtT = const.tile([P, HID], BF16, name="wtT")
        bcol = const.tile([P, 8], F32, name="bcol")
        nbt = const.tile([P, 1], F32, name="nbt")
        def first_half(half):
            cols = slice(half * CH, (half + 1) * CH)
            for j in range(4 * half, 4 * half + 4):
                nc.tensor.transpose(
                    out=hp[:, j * P : (j + 1) * P], in_=htiles[0][:, j, :], identity=identb[:]
                )
            nc.vector.tensor_copy(out=hTs[0][:, cols], in_=hp[:, cols])

        first_half(0)
        nc.tensor.transpose(out=sp[:, 0:P], in_=wtau[:], identity=identb[:])
        nc.tensor.transpose(out=sp[:, P : 2 * P], in_=brow[:], identity=identb[:])
        nc.vector.tensor_copy(out=wtT[:], in_=sp[:, 0:P])
        nc.vector.tensor_scalar_mul(nbt[:], sp[:, P : P + 1], -1.0)
        first_half(1)
        tau_chunk(0)
        h_transposes(1)
        tau_chunk(1)
        h_transposes(2)

        sg = const.tile([P, 2], F32, name="sg")
        kap = const.tile([P, 1], F32, name="kap")
        for u in range(NG):
            if u > 0:
                tau_chunk(2 * u)
                tau_chunk(2 * u + 1)
            if u + 3 < NG:
                h_transposes(u + 3)
            if u in H_AT:
                copy_h(H_AT.index(u))
            if u == W_AT:
                regroup(word_transposes(wraw, 0), wgrp, 0, False)
            if u == W_AT + 1:
                nc.vector.quantize_mx(out=wcodes[:].bitcast(FP8X4), scales=wplane[:], in_=wgrp[:])
            if u in F_AT:
                for k in F_AT[u]:
                    front_step(k)
            if u == 6:
                sp2 = psb.tile([P, P], BF16, name="sp2", tag="b")
                nc.tensor.transpose(out=sp2[:], in_=brow2[:], identity=identb[:])
                nc.vector.tensor_copy(out=bcol[:], in_=sp2[:, 0:8])
            if u == 8:
                nc.scalar.activation(out=sg[:], in_=bcol[:, 2:4], func=ACT.Sigmoid, scale=-1.0)
            if u == 10:
                nc.vector.tensor_tensor(out=kap[:], in0=sg[:, 0:1], in1=sg[:, 1:2], op=ALU.mult)
            if u == 11:
                nc.vector.tensor_scalar_mul(kap[:], kap[:], math.exp(-1e-6))

        sts = {}
        outs = {}

        def gates(c):
            if c % 2 == 0:
                sts[c // 2] = big.tile([P, 4, CH], F32, name="st", tag="big")
            st = sts[c // 2]
            cols = slice((c % 2) * CH, (c % 2 + 1) * CH)
            for i in range(2):
                g = psx.tile([P, CH], F32, name="g", tag="x")
                nc.tensor.matmul_mx(
                    out=g[:],
                    lhsT=wcodes[:, i * HID : (i + 1) * HID].bitcast(FP8X4),
                    lhsT_scale=wplane[:, i * HID : (i + 1) * HID],
                    rhs=codes[c // 2][:, cols].bitcast(FP8X4),
                    rhs_scale=planes[c // 2][:, cols],
                    start=True,
                    stop=True,
                )
                nc.scalar.activation(
                    out=st[:, 2 * i + c % 2, :],
                    in_=g[:],
                    func=(ACT.Sigmoid if i == 0 else ACT.Tanh),
                    bias=bcol[:, i : i + 1],
                )

        def product(c):
            st = sts[c // 2]
            if c // 2 in PAIR_PROD:
                if c % 2 == 1:
                    nc.gpsimd.tensor_tensor(
                        out=st[:, 0:2, :], in0=st[:, 0:2, :], in1=st[:, 2:4, :], op=ALU.mult
                    )
            else:
                a = st[:, c % 2, :]
                eng = nc.vector if c in V_PROD else nc.gpsimd
                eng.tensor_tensor(out=a, in0=a, in1=st[:, 2 + c % 2, :], op=ALU.mult)

        def who(c):
            if c in READY:
                return "R"
            kind = "S" if c >= NCH - TAIL_S else SQ[c % 8]
            return "S" if kind == "D" and c // 2 + G_FIRST >= P_AT else kind

        def square(c):
            if who(c) == "S":
                n = CH - (more(c + 1) if c % 2 == 0 and who(c + 1) == "D" else 0)
                r = tau[c // 4][:, (c % 4) * CH : (c % 4) * CH + n]
                nc.scalar.activation(out=r, in_=r, func=ACT.Square)

        def more(c):
            return MORE if c // 2 % 2 == 1 and who(c - 1) == "S" else 0

        rts = {}
        ats = {}

        def back_r(c):
            r = tau[c // 4][:, (c % 4) * CH : (c % 4 + 1) * CH]
            rts[c] = psb.tile([P, CH], F32, name="rt", tag="b")
            for j in range(4):
                nc.tensor.transpose(
                    out=rts[c][:, j * P : (j + 1) * P],
                    in_=r[:, j * P : (j + 1) * P],
                    identity=identf[:],
                )

        def back_a(c):
            a = sts[c // 2][:, c % 2, :]
            if who(c) == "R" and c % 2 == 0:
                ats[c] = psb.tile([P, CH], F32, name="at", tag="b")
            else:
                ats[c] = psa.tile([P, CH], F32, name="at", tag="a")
            if who(c) == "R":
                nc.tensor.matmul(
                    out=ats[c][:],
                    lhsT=negb[:],
                    rhs=htiles[c // 4][:, (c % 4) * 4 : (c % 4 + 1) * 4, :].rearrange("p s k -> p (s k)"),
                    start=True,
                    stop=False,
                )
            for j in range(4):
                if who(c) == "R":
                    nc.tensor.matmul(
                        out=ats[c][:, j * P : (j + 1) * P],
                        lhsT=a[:, j * P : (j + 1) * P],
                        rhs=identf[:],
                        is_transpose=True,
                        start=False,
                        stop=(j == 3),
                    )
                else:
                    nc.tensor.transpose(
                        out=ats[c][:, j * P : (j + 1) * P],
                        in_=a[:, j * P : (j + 1) * P],
                        identity=identf[:],
                    )

        def numerator(c):
            nums[c] = small.tile([P, CH], F32, name="num", tag="num")
            hn = htiles[c // 4][:, (c % 4) * 4 : (c % 4 + 1) * 4, :].rearrange("p s k -> p (s k)")
            nc.vector.tensor_tensor(out=nums[c][:], in0=ats[c][:], in1=hn, op=ALU.subtract)

        def once(c):
            first = small.tile([P, CH], F32, name="first", tag="first")
            nc.vector.tensor_tensor(out=first[:], in0=rts[c][:], in1=nums[c][:], op=ALU.mult)
            nums[c] = first

        def result(c, alone):
            if c // 4 not in outs:
                outs[c // 4] = mid.tile([P, 4 * CH], F32, name="o", tag="mid", align_bytes=64)
            o = outs[c // 4]
            nc.vector.tensor_tensor(
                out=o[:, (c % 4) * CH : (c % 4 + 1) * CH],
                in0=(ats[c][:] if who(c) == "R" else rts[c][:]),
                in1=(tau_chunk_view(c) if who(c) == "R" else nums[c][:]),
                op=ALU.mult,
            )
            if alone:
                nc.sync.dma_start(
                    out=ov[:, c * 4 : (c + 1) * 4, :],
                    in_=o[:, (c % 4) * CH : (c % 4 + 1) * CH].rearrange("p (s f) -> p s f", f=HID),
                )

        def finish_pair(v):
            c0, c1 = (2 * v, 2 * v + 1) if v < NG - 1 else (2 * v + 1, 2 * v)
            plain = [c for c in (c1, c0) if who(c) != "R"]
            done = [c for c in (c1, c0) if who(c) == "R"]
            for c in (c1, c0):
                back_a(c)
            for c in plain:
                back_r(c)
            for c in (2 * v + 2, 2 * v + 3):
                if c in V_PROD:
                    product(c)
            for c in plain:
                numerator(c)
            for c in done:
                result(c, v >= ALONE)
            twice = [c for c in (c1, c0) if who(c) == "V"]
            for c in twice:
                once(c)
            for c in plain:
                if c not in twice:
                    result(c, v >= ALONE)
            for c in twice:
                result(c, v >= ALONE)
            if v < ALONE:
                nc.sync.dma_start(
                    out=ov[:, v * GS : (v + 1) * GS, :],
                    in_=outs[v // 2][:, (v % 2) * 2 * CH : (v % 2 + 1) * 2 * CH].rearrange(
                        "p (s f) -> p s f", f=HID
                    ),
                )

        nums = {}

        def start_pair(u, products=True):
            gates(2 * u)
            gates(2 * u + 1)
            for c in (2 * u, 2 * u + 1):
                if products and c not in V_PROD:
                    product(c)
            square(2 * u)
            square(2 * u + 1)

        first_steps = sum([len(f) for f in F_AT.values()])
        def after_quantise(g):
            quantise(g)
            if g + NBIG < NG:
                load_comb(g + NBIG)
            if g >= G_FIRST:
                tick = small.tile([P, 1], U32, name="tick", tag="tick")
                nc.gpsimd.tensor_copy(out=tick[:], in_=codes[g][:, 0:1])
            sq = 2 * (g - G_FIRST) + 1
            if sq >= 0 and who(sq) == "D":
                r = tau[sq // 4][:, (sq % 4) * CH - more(sq) : (sq % 4 + 1) * CH]
                nc.gpsimd.tensor_tensor(out=r, in0=r, in1=r, op=ALU.mult)
            if g == P_AT:
                product(0)
                product(1)

        for k in range(2 * NCH):
            if k in jobs_at:
                jobs_at[k][0](jobs_at[k][1])
            if k >= R_STEP and (k - R_STEP) % R_EVERY == 0 and (k - R_STEP) // R_EVERY < len(READY):
                job_ready(READY[(k - R_STEP) // R_EVERY])
            if k >= first_steps:
                front_step(k)
            if k in EARLY:
                start_pair(EARLY.index(k), False)
            if k % 4 == Q_AT and k > Q_AT:
                after_quantise((k - Q_AT) // 4 - 1)
        after_quantise(NG - 1)

        for c in range(2 if P_AT < NG else 0, 2 * len(EARLY)):
            product(c)
        started = len(EARLY)
        for v in range(NG):
            while started < min(NG, v + 1 + (LAG if v < LAG_END else LAG2)):
                start_pair(started)
                started += 1
            finish_pair(v)
